import numpy as np
import ml_dtypes


def mxq(x, axis, fmt="e4m3"):
    dtype, down = {"e4m3": (ml_dtypes.float8_e4m3fn, 7), "e5m2": (ml_dtypes.float8_e5m2, 14)}[fmt]
    v = np.moveaxis(np.asarray(x, np.float32).astype(ml_dtypes.bfloat16).astype(np.float64), axis, -1)
    blocks = v.reshape(v.shape[:-1] + (-1, 32))
    amax = np.abs(blocks).max(-1, keepdims=True)
    byte = np.maximum(np.where(amax > 0, np.frexp(amax)[1] - 1 + 127, 0) - down, 1)
    scale = np.exp2(byte - 127.0)
    codes = (blocks / scale).astype(np.float32).astype(dtype).astype(np.float64)
    return np.moveaxis((codes * scale).reshape(v.shape), -1, axis)


WIDE = False


def mx_kscale(k):
    if not WIDE:
        return np.ones(k)
    levels = np.array([10, -10, 5, -5, 0])
    a = np.random.permutation(np.resize(levels, k // 512 * 4)).reshape(k // 512, 4)
    idx = np.arange(k)
    return np.exp2(a[idx // 512, idx % 128 // 32])


BF16 = ml_dtypes.bfloat16


def bf(x):
    return np.asarray(x, np.float32).astype(BF16)


def f64(x):
    return np.asarray(x).astype(np.float64)


E2M1 = np.array([0.0, 0.5, 1.0, 1.5, 2.0, 3.0, 4.0, 6.0, -0.0, -0.5, -1.0, -1.5, -2.0, -3.0, -4.0, -6.0])


def pack_weight(w, fmt):
    k, n = w.shape
    w = f64(bf(w)).reshape(k // 32, 32, n)
    amax = np.abs(w).max(1)
    if fmt == "e4m3":
        byte = np.frexp(amax)[1] - 1 + 127 - 7
    else:
        mant, ex = np.frexp(amax / 6.0)
        byte = np.where(mant > 0.5, ex, ex - 1) + 127
    byte = np.clip(np.where(amax > 0, byte, 1), 1, 254)
    scaled = (w * np.exp2(127.0 - byte)[:, None, :]).reshape(k, n).astype(np.float32)
    by_word = np.ascontiguousarray(scaled.reshape(k // 512, 128, 4, n).transpose(0, 1, 3, 2))
    if fmt == "e4m3":
        words = by_word.astype(ml_dtypes.float8_e4m3fn).view(np.uint8)
    else:
        c = by_word.astype(ml_dtypes.float4_e2m1fn).view(np.uint8) & 0xF
        words = c[..., 0::2] | (c[..., 1::2] << 4)
    return np.ascontiguousarray(words), np.ascontiguousarray(byte.astype(np.uint8).reshape(k // 512, 16, n))


def unpack_weight(words, scales, fmt):
    g, p, n, _ = words.shape
    if fmt == "e4m3":
        vals = np.ascontiguousarray(words).view(ml_dtypes.float8_e4m3fn).astype(np.float64)
    else:
        nib = np.empty((g, p, n, 4), np.uint8)
        nib[..., 0::2] = words & 0xF
        nib[..., 1::2] = words >> 4
        vals = E2M1[nib]
    vals = vals * np.repeat(np.exp2(scales.astype(np.float64) - 127.0), 8, axis=1)[..., None]
    return vals.transpose(0, 1, 3, 2).reshape(g * 512, n)


B, D, C, NP, NS = 256, 8192, 512, 512, 512
ALPHA_NEG = 1.0 / 10.0
FMT = "e4m3"


def relu(v):
    return np.maximum(v, 0.0)


def setup_inputs():
    t = mx_kscale(NP)
    u = mx_kscale(NS)
    x_batch = bf(np.random.uniform(size=(B, D)))
    predicted = bf(np.random.standard_normal((B, D)))
    r_som = bf(np.maximum(np.random.standard_normal((B, NS)), 0.0) * 1.1 * u)
    r_neg_batch = bf(np.random.uniform(size=(B, D)) * 0.5)
    w_ff = np.random.standard_normal((NP, D)) * 1.5 / np.sqrt(D) * t[:, None]
    w_inh = np.random.standard_normal((D, NP)) * 1.2 / np.sqrt(NP) / t
    w_som = np.random.standard_normal((D, NS)) * 0.9 / np.sqrt(NS) / u
    ff_words, ff_scales = pack_weight(np.ascontiguousarray(w_ff.T), FMT)
    inh_words, inh_scales = pack_weight(np.ascontiguousarray(w_inh.T), FMT)
    som_words, som_scales = pack_weight(np.ascontiguousarray(w_som.T), FMT)
    return {
        "x_batch": x_batch,
        "predicted": predicted,
        "r_som": r_som,
        "r_neg_batch": r_neg_batch,
        "W_pv1_ff_words": ff_words,
        "W_pv1_ff_scales": ff_scales,
        "W_inh_pe_neg_words": inh_words,
        "W_inh_pe_neg_scales": inh_scales,
        "W_som_dend_words": som_words,
        "W_som_dend_scales": som_scales,
    }


def reference(x_batch, predicted, r_som, r_neg_batch, W_pv1_ff_words, W_pv1_ff_scales, W_inh_pe_neg_words, W_inh_pe_neg_scales, W_som_dend_words, W_som_dend_scales):
    xf, pf = f64(x_batch), f64(predicted)
    r_pv1 = relu(mxq(xf, 1, "e4m3") @ unpack_weight(W_pv1_ff_words, W_pv1_ff_scales, FMT))
    inh_pv = mxq(r_pv1, 1, "e4m3") @ unpack_weight(W_inh_pe_neg_words, W_inh_pe_neg_scales, FMT)
    inh_som = mxq(f64(r_som), 1, "e4m3") @ unpack_weight(W_som_dend_words, W_som_dend_scales, FMT)
    pe_neg = relu(pf - xf - inh_pv - inh_som)
    return (1.0 - ALPHA_NEG) * f64(r_neg_batch) + ALPHA_NEG * pe_neg

@@ -1,0 +1,274 @@
+from contextlib import ExitStack
+
+import concourse.mybir as mybir
+from concourse.masks import make_identity
+
+F32 = mybir.dt.float32
+BF16 = mybir.dt.bfloat16
+I32 = mybir.dt.int32
+U32 = mybir.dt.uint32
+U8 = mybir.dt.uint8
+FP8X4 = mybir.dt.float8_e4m3fn_x4
+ALU = mybir.AluOpType
+ACT = mybir.ActivationFunctionType
+
+P = 128
+PACK = 4
+K_PASS = P * PACK
+BANK = 512
+
+BATCH = 256
+B_TILES = BATCH // P
+D = 8192
+HIDDEN = 512
+ALPHA = 1.0 / 10.0
+
+WIDE = 2048
+STEPS = D // WIDE
+GROUPS = WIDE // K_PASS
+HALF = 2 * BANK
+HALVES = B_TILES * D // HALF
+HALVES_PER_SLAB = B_TILES * WIDE // HALF
+AHEAD = 3
+LAG = 2
+QUADS = 4
+ROWS = 4
+
+FLOPS = 2 * BATCH * D * HIDDEN * 3
+
+
+def quantise_group(nc, flip_pool, stage, ident_f32, rows, codes, plane):
+    flipped = flip_pool.tile([P, 2, BATCH], F32, name="flipped", tag="flip")
+    for b in range(B_TILES):
+        words = rows[b].bitcast(F32)
+        for u in range(2):
+            nc.tensor.transpose(flipped[:, u, b * P : (b + 1) * P], words[:, u : K_PASS // 2 : 2], ident_f32)
+    grouped = stage.tile([P, BATCH, PACK], BF16, name="grouped", align_bytes=64)
+    nc.scalar.copy(out=grouped[:].bitcast(F32), in_=flipped[:].rearrange("p u c -> p c u"))
+    nc.vector.quantize_mx(
+        out=codes.bitcast(FP8X4), scales=plane, in_=grouped[:].rearrange("p c t -> p (c t)")
+    )
+
+
+def tile_pecircuits_pb_k_kernel(
+    tc,
+    x_batch,
+    predicted,
+    r_som,
+    r_neg_batch,
+    W_pv1_ff_words,
+    W_pv1_ff_scales,
+    W_inh_pe_neg_words,
+    W_inh_pe_neg_scales,
+    W_som_dend_words,
+    W_som_dend_scales,
+    out,
+):
+    nc = tc.nc
+    x_view = x_batch.rearrange("(b p) k -> p b k", p=P)
+    pred_view = predicted.rearrange("(b p) k -> p b k", p=P)
+    rneg_view = r_neg_batch.rearrange("(b p) k -> p b k", p=P)
+    out_view = out.rearrange("(b p) k -> p b k", p=P)
+    inh_view = W_inh_pe_neg_words[0].rearrange("p n t -> p (n t)")
+    som_view = W_som_dend_words[0].rearrange("p n t -> p (n t)")
+
+    with ExitStack() as ctx:
+        ctx.enter_context(tc.manual_schedule())
+        keep = ctx.enter_context(tc.tile_pool(name="keep", bufs=1))
+        x_pool = ctx.enter_context(tc.tile_pool(name="x_pool", bufs=3))
+        ff_pool = ctx.enter_context(tc.tile_pool(name="ff_pool", bufs=2))
+        stage = ctx.enter_context(tc.tile_pool(name="stage", bufs=GROUPS))
+        slab_pool = ctx.enter_context(tc.tile_pool(name="slab_pool", bufs=AHEAD))
+        sum1_pool = ctx.enter_context(tc.psum_pool(name="sum1_pool", bufs=1))
+        flip_pool = ctx.enter_context(tc.psum_pool(name="flip_pool", bufs=3))
+        sum2_pool = ctx.enter_context(tc.psum_pool(name="sum2_pool", bufs=3))
+
+        ff_planes = keep.tile([P, STEPS, HIDDEN], U8, name="ff_planes", align_bytes=64)
+        out_planes = keep.tile([P, D // 2], U8, name="out_planes", align_bytes=64)
+        nc.vector.memset(ff_planes[:].bitcast(I32), 0)
+        nc.vector.memset(out_planes[:].bitcast(I32), 0)
+
+        ident_f32 = keep.tile([P, P], F32, name="ident_f32")
+        ident_bf16 = keep.tile([P, P], BF16, name="ident_bf16")
+        make_identity(nc, ident_f32[:])
+        make_identity(nc, ident_bf16[:])
+
+        x_tiles = {}
+        pred_tiles = {}
+        ff_tiles = {}
+
+        def load_step(s):
+            cols = slice(s * WIDE, (s + 1) * WIDE)
+            x_tiles[s] = x_pool.tile([P, B_TILES, WIDE], BF16, name="x_slab")
+            nc.sync.dma_start(out=x_tiles[s][:], in_=x_view[:, :, cols])
+            for quad in range(QUADS):
+                nc.sync.dma_start(
+                    out=ff_planes[32 * quad : 32 * quad + GROUPS * ROWS, s, :].bitcast(I32),
+                    in_=W_pv1_ff_scales[
+                        s * GROUPS : (s + 1) * GROUPS, quad * ROWS : (quad + 1) * ROWS, :
+                    ].bitcast(I32),
+                )
+            ff_tiles[s] = ff_pool.tile([P, GROUPS, HIDDEN], U32, name="ff_words")
+            nc.sync.dma_start(
+                out=ff_tiles[s][:].bitcast(I32),
+                in_=W_pv1_ff_words[s * GROUPS : (s + 1) * GROUPS]
+                .rearrange("g p n t -> p g (n t)")
+                .bitcast(I32),
+            )
+            for w, scales in enumerate((W_inh_pe_neg_scales, W_som_dend_scales)):
+                first = 32 * s + 2 * ROWS * w
+                nc.sync.dma_start(
+                    out=out_planes[first : first + 2 * ROWS, :].bitcast(I32),
+                    in_=scales[0, s * ROWS : (s + 1) * ROWS, :]
+                    .rearrange("r (h n) -> h r n", h=2)
+                    .bitcast(I32),
+                )
+            pred_tiles[s] = x_pool.tile([P, B_TILES, WIDE], BF16, name="pred_slab")
+            nc.sync.dma_start(out=pred_tiles[s][:], in_=pred_view[:, :, cols])
+
+        slabs = {}
+
+        def load_slab(j):
+            som_words = slab_pool.tile([P, WIDE], U32, name="som_words", align_bytes=64)
+            inh_words = slab_pool.tile([P, WIDE], U32, name="inh_words", align_bytes=64)
+            rneg = slab_pool.tile([P, B_TILES, WIDE], BF16, name="rneg")
+            byte_cols = slice(j * WIDE * PACK, (j + 1) * WIDE * PACK)
+            nc.sync.dma_start(out=som_words[:].bitcast(I32), in_=som_view[:, byte_cols].bitcast(I32))
+            nc.sync.dma_start(out=inh_words[:].bitcast(I32), in_=inh_view[:, byte_cols].bitcast(I32))
+            nc.sync.dma_start(out=rneg[:], in_=rneg_view[:, :, j * WIDE : (j + 1) * WIDE])
+            slabs[j] = (som_words, inh_words, rneg)
+
+        work = [keep.tile([P, B_TILES, WIDE], F32, name="work%d" % s) for s in range(STEPS)]
+
+        def difference(s):
+            for b in range(B_TILES):
+                nc.vector.tensor_tensor(
+                    out=work[s][:, b, :],
+                    in0=pred_tiles[s][:, b, :],
+                    in1=x_tiles[s][:, b, :],
+                    op=ALU.subtract,
+                )
+
+        load_step(0)
+        som_rows = keep.tile([P, B_TILES, HIDDEN], BF16, name="som_rows")
+        nc.sync.dma_start(out=som_rows[:], in_=r_som.rearrange("(b p) k -> p b k", p=P))
+        load_step(1)
+
+        hidden_sum = [sum1_pool.tile([P, HIDDEN], F32, name="hidden_sum%d" % b) for b in range(B_TILES)]
+        som_codes = keep.tile([P, BATCH], U32, name="som_codes", align_bytes=64)
+        som_plane = keep.tile([P, BATCH], U8, name="som_plane", align_bytes=64)
+        pv_codes = keep.tile([P, BATCH], U32, name="pv_codes", align_bytes=64)
+        pv_plane = keep.tile([P, BATCH], U8, name="pv_plane", align_bytes=64)
+
+        for s in range(STEPS):
+            x_codes = []
+            x_planes = []
+            if s == 1:
+                rows = [som_rows[:, b, :] for b in range(B_TILES)]
+                quantise_group(nc, flip_pool, stage, ident_f32[:], rows, som_codes[:], som_plane[:])
+            for i in range(GROUPS):
+                x_codes.append(stage.tile([P, BATCH], U32, name="x_codes", align_bytes=64))
+                x_planes.append(stage.tile([P, BATCH], U8, name="x_plane", align_bytes=64))
+                rows = [x_tiles[s][:, b, i * K_PASS : (i + 1) * K_PASS] for b in range(B_TILES)]
+                quantise_group(nc, flip_pool, stage, ident_f32[:], rows, x_codes[i][:], x_planes[i][:])
+            for i in range(GROUPS):
+                for b in range(B_TILES):
+                    batch_cols = slice(b * P, (b + 1) * P)
+                    nc.tensor.matmul_mx(
+                        out=hidden_sum[b][:],
+                        lhsT=x_codes[i][:, batch_cols].bitcast(FP8X4),
+                        lhsT_scale=x_planes[i][:, batch_cols],
+                        rhs=ff_tiles[s][:, i, :].bitcast(FP8X4),
+                        rhs_scale=ff_planes[ROWS * i : P, s, :],
+                        start=(s == 0 and i == 0),
+                        stop=(s == STEPS - 1 and i == GROUPS - 1),
+                    )
+            if s > 0:
+                difference(s - 1)
+            if s + 2 < STEPS:
+                load_step(s + 2)
+        for j in range(AHEAD):
+            load_slab(j)
+
+        rates = [keep.tile([P, PACK, P], BF16, name="rates%d" % b) for b in range(B_TILES)]
+        for b in range(B_TILES):
+            nc.scalar.activation(
+                out=rates[b][:],
+                in_=hidden_sum[b][:].rearrange("r (p t) -> r t p", t=PACK),
+                func=ACT.Relu,
+            )
+        turned = []
+        for b in range(B_TILES):
+            turned.append(flip_pool.tile([P, PACK, P], BF16, name="turned", tag="flip"))
+            for t in range(PACK):
+                nc.tensor.transpose(turned[b][:, t, :], rates[b][:, t, :], ident_bf16[:])
+        for b in range(B_TILES):
+            batch_cols = slice(b * P, (b + 1) * P)
+            pv_grouped = keep.tile([P, P, PACK], BF16, name="pv_grouped%d" % b, align_bytes=64)
+            nc.scalar.copy(out=pv_grouped[:], in_=turned[b][:].rearrange("p t r -> p r t"))
+            nc.vector.quantize_mx(
+                out=pv_codes[:, batch_cols].bitcast(FP8X4),
+                scales=pv_plane[:, batch_cols],
+                in_=pv_grouped[:].rearrange("p r t -> p (r t)"),
+            )
+        difference(STEPS - 1)
+
+        def place(k):
+            j, rest = divmod(k, HALVES_PER_SLAB)
+            b, h = divmod(rest, WIDE // HALF)
+            return j, b, h * HALF
+
+        for k in range(HALVES + LAG):
+            if k < HALVES:
+                j, b, first = place(k)
+                som_words, inh_words, rneg = slabs[j]
+                batch_cols = slice(b * P, (b + 1) * P)
+                side = j // (STEPS // 2)
+                for c in range(HALF // BANK):
+                    cols = slice(first + c * BANK, first + (c + 1) * BANK)
+                    plane_first = (j % (STEPS // 2)) * WIDE + first + c * BANK
+                    plane_cols = slice(plane_first, plane_first + BANK)
+                    inhibition = sum2_pool.tile([P, BANK], F32, name="inhibition")
+                    nc.tensor.matmul_mx(
+                        out=inhibition[:],
+                        lhsT=som_codes[:, batch_cols].bitcast(FP8X4),
+                        lhsT_scale=som_plane[:, batch_cols],
+                        rhs=som_words[:, cols].bitcast(FP8X4),
+                        rhs_scale=out_planes[ROWS * (2 + side) : P, plane_cols],
+                        start=True,
+                        stop=False,
+                    )
+                    nc.tensor.matmul_mx(
+                        out=inhibition[:],
+                        lhsT=pv_codes[:, batch_cols].bitcast(FP8X4),
+                        lhsT_scale=pv_plane[:, batch_cols],
+                        rhs=inh_words[:, cols].bitcast(FP8X4),
+                        rhs_scale=out_planes[ROWS * side : P, plane_cols],
+                        start=False,
+                        stop=True,
+                    )
+                    nc.vector.tensor_tensor(
+                        out=work[j][:, b, cols], in0=work[j][:, b, cols], in1=inhibition[:], op=ALU.subtract
+                    )
+                half_cols = slice(first, first + HALF)
+                nc.scalar.activation(
+                    out=work[j][:, b, half_cols], in_=work[j][:, b, half_cols], func=ACT.Relu, scale=ALPHA
+                )
+            if k >= LAG:
+                j, b, first = place(k - LAG)
+                rneg = slabs[j][2]
+                half_cols = slice(first, first + HALF)
+                nc.vector.scalar_tensor_tensor(
+                    out=work[j][:, b, half_cols],
+                    in0=rneg[:, b, half_cols],
+                    scalar=1.0 - ALPHA,
+                    in1=work[j][:, b, half_cols],
+                    op0=ALU.mult,
+                    op1=ALU.add,
+                )
+                nc.sync.dma_start(
+                    out=out_view[:, b, j * WIDE + first : j * WIDE + first + HALF],
+                    in_=work[j][:, b, half_cols],
+                )
+                if (k - LAG) % HALVES_PER_SLAB == HALVES_PER_SLAB - 1 and j + AHEAD < STEPS:
+                    load_slab(j + AHEAD)

@@ -31,6 +31,7 @@ HALVES = B_TILES * D // HALF
 HALVES_PER_SLAB = B_TILES * WIDE // HALF
 AHEAD = 3
 LAG = 2
+VECTOR_SLABS = 2
 QUADS = 4
 ROWS = 4
 
@@ -92,6 +93,8 @@ def tile_pecircuits_pb_k_kernel(
         ident_bf16 = keep.tile([P, P], BF16, name="ident_bf16")
         make_identity(nc, ident_f32[:])
         make_identity(nc, ident_bf16[:])
+        minus_ident = keep.tile([P, P], BF16, name="minus_ident")
+        nc.vector.tensor_scalar_mul(out=minus_ident[:], in0=ident_bf16[:], scalar1=-1.0)
 
         x_tiles = {}
         pred_tiles = {}
@@ -123,8 +126,10 @@ def tile_pecircuits_pb_k_kernel(
                     .rearrange("r (h n) -> h r n", h=2)
                     .bitcast(I32),
                 )
+
+        def load_predicted(s):
             pred_tiles[s] = x_pool.tile([P, B_TILES, WIDE], BF16, name="pred_slab")
-            nc.sync.dma_start(out=pred_tiles[s][:], in_=pred_view[:, :, cols])
+            nc.sync.dma_start(out=pred_tiles[s][:], in_=pred_view[:, :, s * WIDE : (s + 1) * WIDE])
 
         slabs = {}
 
@@ -150,9 +155,11 @@ def tile_pecircuits_pb_k_kernel(
                 )
 
         load_step(0)
+        load_predicted(0)
         som_rows = keep.tile([P, B_TILES, HIDDEN], BF16, name="som_rows")
         nc.sync.dma_start(out=som_rows[:], in_=r_som.rearrange("(b p) k -> p b k", p=P))
         load_step(1)
+        load_predicted(1)
 
         hidden_sum = [sum1_pool.tile([P, HIDDEN], F32, name="hidden_sum%d" % b) for b in range(B_TILES)]
         som_codes = keep.tile([P, BATCH], U32, name="som_codes", align_bytes=64)
@@ -183,10 +190,12 @@ def tile_pecircuits_pb_k_kernel(
                         start=(s == 0 and i == 0),
                         stop=(s == STEPS - 1 and i == GROUPS - 1),
                     )
-            if s > 0:
-                difference(s - 1)
+            if s < VECTOR_SLABS:
+                difference(s)
             if s + 2 < STEPS:
                 load_step(s + 2)
+        for s in range(VECTOR_SLABS, STEPS):
+            load_predicted(s)
         for j in range(AHEAD):
             load_slab(j)
 
@@ -211,12 +220,20 @@ def tile_pecircuits_pb_k_kernel(
                 scales=pv_plane[:, batch_cols],
                 in_=pv_grouped[:].rearrange("p r t -> p (r t)"),
             )
-        difference(STEPS - 1)
 
         def place(k):
             j, rest = divmod(k, HALVES_PER_SLAB)
             b, h = divmod(rest, WIDE // HALF)
             return j, b, h * HALF
+
+        def difference_by_tensor(k):
+            j, b, first = place(k)
+            for c in range(HALF // BANK):
+                cols = slice(first + c * BANK, first + (c + 1) * BANK)
+                gap = flip_pool.tile([P, BANK], F32, name="gap", tag="flip")
+                nc.tensor.matmul(out=gap[:], lhsT=ident_bf16[:], rhs=pred_tiles[j][:, b, cols], start=True, stop=False)
+                nc.tensor.matmul(out=gap[:], lhsT=minus_ident[:], rhs=x_tiles[j][:, b, cols], start=False, stop=True)
+                nc.scalar.copy(out=work[j][:, b, cols], in_=gap[:])
 
         for k in range(HALVES + LAG):
             if k < HALVES:
@@ -250,6 +267,8 @@ def tile_pecircuits_pb_k_kernel(
                     nc.vector.tensor_tensor(
                         out=work[j][:, b, cols], in0=work[j][:, b, cols], in1=inhibition[:], op=ALU.subtract
                     )
+                if k + VECTOR_SLABS * HALVES_PER_SLAB < HALVES:
+                    difference_by_tensor(k + VECTOR_SLABS * HALVES_PER_SLAB)
                 half_cols = slice(first, first + HALF)
                 nc.scalar.activation(
                     out=work[j][:, b, half_cols], in_=work[j][:, b, half_cols], func=ACT.Relu, scale=ALPHA

@@ -194,10 +194,10 @@ def tile_pecircuits_pb_k_kernel(
                 difference(s)
             if s + 2 < STEPS:
                 load_step(s + 2)
-        for s in range(VECTOR_SLABS, STEPS):
-            load_predicted(s)
         for j in range(AHEAD):
             load_slab(j)
+            if VECTOR_SLABS + j < STEPS:
+                load_predicted(VECTOR_SLABS + j)
 
         rates = [keep.tile([P, PACK, P], BF16, name="rates%d" % b) for b in range(B_TILES)]
         for b in range(B_TILES):
@@ -267,8 +267,8 @@ def tile_pecircuits_pb_k_kernel(
                     nc.vector.tensor_tensor(
                         out=work[j][:, b, cols], in0=work[j][:, b, cols], in1=inhibition[:], op=ALU.subtract
                     )
-                if k + VECTOR_SLABS * HALVES_PER_SLAB < HALVES:
-                    difference_by_tensor(k + VECTOR_SLABS * HALVES_PER_SLAB)
+                if VECTOR_SLABS * HALVES_PER_SLAB <= k + HALVES_PER_SLAB < HALVES:
+                    difference_by_tensor(k + HALVES_PER_SLAB)
                 half_cols = slice(first, first + HALF)
                 nc.scalar.activation(
                     out=work[j][:, b, half_cols], in_=work[j][:, b, half_cols], func=ACT.Relu, scale=ALPHA

@@ -26,10 +26,13 @@ ALPHA = 1.0 / 10.0
 WIDE = 2048
 STEPS = D // WIDE
 GROUPS = WIDE // K_PASS
+ROW = 2 * WIDE
+SIDES = D // ROW
 HALF = 2 * BANK
 HALVES = B_TILES * D // HALF
 HALVES_PER_SLAB = B_TILES * WIDE // HALF
-AHEAD = 3
+PIECES = WIDE // HALF
+RING = 14
 LAG = 2
 VECTOR_SLABS = 2
 QUADS = 4
@@ -66,9 +69,6 @@ def tile_pecircuits_pb_k_kernel(
     out,
 ):
     nc = tc.nc
-    x_view = x_batch.rearrange("(b p) k -> p b k", p=P)
-    pred_view = predicted.rearrange("(b p) k -> p b k", p=P)
-    rneg_view = r_neg_batch.rearrange("(b p) k -> p b k", p=P)
     out_view = out.rearrange("(b p) k -> p b k", p=P)
     inh_view = W_inh_pe_neg_words[0].rearrange("p n t -> p (n t)")
     som_view = W_som_dend_words[0].rearrange("p n t -> p (n t)")
@@ -76,18 +76,18 @@ def tile_pecircuits_pb_k_kernel(
     with ExitStack() as ctx:
         ctx.enter_context(tc.manual_schedule())
         keep = ctx.enter_context(tc.tile_pool(name="keep", bufs=1))
-        x_pool = ctx.enter_context(tc.tile_pool(name="x_pool", bufs=3))
-        ff_pool = ctx.enter_context(tc.tile_pool(name="ff_pool", bufs=2))
+        ring = ctx.enter_context(tc.tile_pool(name="ring", bufs=RING))
         stage = ctx.enter_context(tc.tile_pool(name="stage", bufs=GROUPS))
-        slab_pool = ctx.enter_context(tc.tile_pool(name="slab_pool", bufs=AHEAD))
         sum1_pool = ctx.enter_context(tc.psum_pool(name="sum1_pool", bufs=1))
         flip_pool = ctx.enter_context(tc.psum_pool(name="flip_pool", bufs=3))
         sum2_pool = ctx.enter_context(tc.psum_pool(name="sum2_pool", bufs=3))
 
         ff_planes = keep.tile([P, STEPS, HIDDEN], U8, name="ff_planes", align_bytes=64)
-        out_planes = keep.tile([P, D // 2], U8, name="out_planes", align_bytes=64)
+        inh_planes = keep.tile([P, WIDE], U8, name="inh_planes", align_bytes=64)
+        som_planes = keep.tile([P, WIDE], U8, name="som_planes", align_bytes=64)
         nc.vector.memset(ff_planes[:].bitcast(I32), 0)
-        nc.vector.memset(out_planes[:].bitcast(I32), 0)
+        nc.vector.memset(inh_planes[:].bitcast(I32), 0)
+        nc.vector.memset(som_planes[:].bitcast(I32), 0)
 
         ident_f32 = keep.tile([P, P], F32, name="ident_f32")
         ident_bf16 = keep.tile([P, P], BF16, name="ident_bf16")
@@ -98,12 +98,28 @@ def tile_pecircuits_pb_k_kernel(
 
         x_tiles = {}
         pred_tiles = {}
+        rneg_tiles = {}
         ff_tiles = {}
+        weight_tiles = {}
 
-        def load_step(s):
-            cols = slice(s * WIDE, (s + 1) * WIDE)
-            x_tiles[s] = x_pool.tile([P, B_TILES, WIDE], BF16, name="x_slab")
-            nc.sync.dma_start(out=x_tiles[s][:], in_=x_view[:, :, cols])
+        def load_rows(tiles, b, side, dram, tile):
+            tiles[b, side] = tile
+            nc.sync.dma_start(out=tile[:], in_=dram[b * P : (b + 1) * P, side * ROW : (side + 1) * ROW])
+
+        def ring_rows(tiles, b, side, dram):
+            rows = ring.tile([P, ROW], BF16, name="rows", tag="ring", align_bytes=64)
+            load_rows(tiles, b, side, dram, rows)
+
+        def load_ff(s):
+            ff_tiles[s] = ring.tile([P, GROUPS, HIDDEN], U32, name="ff_words", tag="ring", align_bytes=64)
+            nc.sync.dma_start(
+                out=ff_tiles[s][:].bitcast(I32),
+                in_=W_pv1_ff_words[s * GROUPS : (s + 1) * GROUPS]
+                .rearrange("g p n t -> p g (n t)")
+                .bitcast(I32),
+            )
+
+        def load_ff_scales(s):
             for quad in range(QUADS):
                 nc.sync.dma_start(
                     out=ff_planes[32 * quad : 32 * quad + GROUPS * ROWS, s, :].bitcast(I32),
@@ -111,55 +127,64 @@ def tile_pecircuits_pb_k_kernel(
                         s * GROUPS : (s + 1) * GROUPS, quad * ROWS : (quad + 1) * ROWS, :
                     ].bitcast(I32),
                 )
-            ff_tiles[s] = ff_pool.tile([P, GROUPS, HIDDEN], U32, name="ff_words")
-            nc.sync.dma_start(
-                out=ff_tiles[s][:].bitcast(I32),
-                in_=W_pv1_ff_words[s * GROUPS : (s + 1) * GROUPS]
-                .rearrange("g p n t -> p g (n t)")
-                .bitcast(I32),
-            )
-            for w, scales in enumerate((W_inh_pe_neg_scales, W_som_dend_scales)):
-                first = 32 * s + 2 * ROWS * w
+
+        def load_out_scales(quad):
+            for planes, scales in ((som_planes, W_som_dend_scales), (inh_planes, W_inh_pe_neg_scales)):
                 nc.sync.dma_start(
-                    out=out_planes[first : first + 2 * ROWS, :].bitcast(I32),
-                    in_=scales[0, s * ROWS : (s + 1) * ROWS, :]
-                    .rearrange("r (h n) -> h r n", h=2)
+                    out=planes[32 * quad : 32 * quad + STEPS * ROWS, :].bitcast(I32),
+                    in_=scales[0, quad * ROWS : (quad + 1) * ROWS, :]
+                    .rearrange("r (h n) -> h r n", h=STEPS)
                     .bitcast(I32),
                 )
 
-        def load_predicted(s):
-            pred_tiles[s] = x_pool.tile([P, B_TILES, WIDE], BF16, name="pred_slab")
-            nc.sync.dma_start(out=pred_tiles[s][:], in_=pred_view[:, :, s * WIDE : (s + 1) * WIDE])
-
-        slabs = {}
-
-        def load_slab(j):
-            som_words = slab_pool.tile([P, WIDE], U32, name="som_words", align_bytes=64)
-            inh_words = slab_pool.tile([P, WIDE], U32, name="inh_words", align_bytes=64)
-            rneg = slab_pool.tile([P, B_TILES, WIDE], BF16, name="rneg")
+        def load_weights(j):
             byte_cols = slice(j * WIDE * PACK, (j + 1) * WIDE * PACK)
-            nc.sync.dma_start(out=som_words[:].bitcast(I32), in_=som_view[:, byte_cols].bitcast(I32))
-            nc.sync.dma_start(out=inh_words[:].bitcast(I32), in_=inh_view[:, byte_cols].bitcast(I32))
-            nc.sync.dma_start(out=rneg[:], in_=rneg_view[:, :, j * WIDE : (j + 1) * WIDE])
-            slabs[j] = (som_words, inh_words, rneg)
+            pair = []
+            for view in (som_view, inh_view):
+                words = ring.tile([P, WIDE], U32, name="words", tag="ring", align_bytes=64)
+                nc.sync.dma_start(out=words[:].bitcast(I32), in_=view[:, byte_cols].bitcast(I32))
+                pair.append(words)
+            weight_tiles[j] = pair
 
         work = [keep.tile([P, B_TILES, WIDE], F32, name="work%d" % s) for s in range(STEPS)]
 
-        def difference(s):
-            for b in range(B_TILES):
-                nc.vector.tensor_tensor(
-                    out=work[s][:, b, :],
-                    in0=pred_tiles[s][:, b, :],
-                    in1=x_tiles[s][:, b, :],
-                    op=ALU.subtract,
-                )
+        def side_cols(s):
+            first = s * WIDE % ROW
+            return s * WIDE // ROW, slice(first, first + WIDE)
 
-        load_step(0)
-        load_predicted(0)
+        def difference(s, b):
+            side, cols = side_cols(s)
+            nc.vector.tensor_tensor(
+                out=work[s][:, b, :],
+                in0=pred_tiles[b, side][:, cols],
+                in1=x_tiles[b, side][:, cols],
+                op=ALU.subtract,
+            )
+
+        ring_rows(x_tiles, 0, 0, x_batch)
+        load_ff_scales(0)
+        ring_rows(x_tiles, 1, 0, x_batch)
+        load_ff(0)
+        load_ff_scales(1)
+        load_ff(1)
         som_rows = keep.tile([P, B_TILES, HIDDEN], BF16, name="som_rows")
         nc.sync.dma_start(out=som_rows[:], in_=r_som.rearrange("(b p) k -> p b k", p=P))
-        load_step(1)
-        load_predicted(1)
+        ring_rows(pred_tiles, 0, 0, predicted)
+        load_ff_scales(2)
+        ring_rows(pred_tiles, 1, 0, predicted)
+        load_ff_scales(3)
+        for b in range(B_TILES):
+            kept = keep.tile([P, ROW], BF16, name="x_kept%d" % b)
+            load_rows(x_tiles, b, 1, x_batch, kept)
+            load_out_scales(2 * b)
+        load_ff(2)
+        load_out_scales(1)
+        load_ff(3)
+        load_out_scales(3)
+        load_weights(0)
+        for b in range(B_TILES):
+            ring_rows(rneg_tiles, b, 0, r_neg_batch)
+        load_weights(1)
 
         hidden_sum = [sum1_pool.tile([P, HIDDEN], F32, name="hidden_sum%d" % b) for b in range(B_TILES)]
         som_codes = keep.tile([P, BATCH], U32, name="som_codes", align_bytes=64)
@@ -170,13 +195,15 @@ def tile_pecircuits_pb_k_kernel(
         for s in range(STEPS):
             x_codes = []
             x_planes = []
-            if s == 1:
+            if s == 2:
                 rows = [som_rows[:, b, :] for b in range(B_TILES)]
                 quantise_group(nc, flip_pool, stage, ident_f32[:], rows, som_codes[:], som_plane[:])
+            side, slab_cols = side_cols(s)
             for i in range(GROUPS):
                 x_codes.append(stage.tile([P, BATCH], U32, name="x_codes", align_bytes=64))
                 x_planes.append(stage.tile([P, BATCH], U8, name="x_plane", align_bytes=64))
-                rows = [x_tiles[s][:, b, i * K_PASS : (i + 1) * K_PASS] for b in range(B_TILES)]
+                first = slab_cols.start + i * K_PASS
+                rows = [x_tiles[b, side][:, first : first + K_PASS] for b in range(B_TILES)]
                 quantise_group(nc, flip_pool, stage, ident_f32[:], rows, x_codes[i][:], x_planes[i][:])
             for i in range(GROUPS):
                 for b in range(B_TILES):
@@ -190,14 +217,16 @@ def tile_pecircuits_pb_k_kernel(
                         start=(s == 0 and i == 0),
                         stop=(s == STEPS - 1 and i == GROUPS - 1),
                     )
-            if s < VECTOR_SLABS:
-                difference(s)
-            if s + 2 < STEPS:
-                load_step(s + 2)
-        for j in range(AHEAD):
-            load_slab(j)
-            if VECTOR_SLABS + j < STEPS:
-                load_predicted(VECTOR_SLABS + j)
+            if s >= 1 and s - 1 < VECTOR_SLABS:
+                for b in range(B_TILES):
+                    difference(s - 1, b)
+
+        for b in range(B_TILES):
+            ring_rows(pred_tiles, b, 1, predicted)
+        load_weights(2)
+        for b in range(B_TILES):
+            ring_rows(rneg_tiles, b, 1, r_neg_batch)
+        load_weights(3)
 
         rates = [keep.tile([P, PACK, P], BF16, name="rates%d" % b) for b in range(B_TILES)]
         for b in range(B_TILES):
@@ -223,35 +252,39 @@ def tile_pecircuits_pb_k_kernel(
 
         def place(k):
             j, rest = divmod(k, HALVES_PER_SLAB)
-            b, h = divmod(rest, WIDE // HALF)
+            b, h = divmod(rest, PIECES)
             return j, b, h * HALF
 
         def difference_by_tensor(k):
             j, b, first = place(k)
+            side, slab_cols = side_cols(j)
             for c in range(HALF // BANK):
-                cols = slice(first + c * BANK, first + (c + 1) * BANK)
+                start = first + c * BANK
+                cols = slice(start, start + BANK)
+                row_cols = slice(slab_cols.start + start, slab_cols.start + start + BANK)
                 gap = flip_pool.tile([P, BANK], F32, name="gap", tag="flip")
-                nc.tensor.matmul(out=gap[:], lhsT=ident_bf16[:], rhs=pred_tiles[j][:, b, cols], start=True, stop=False)
-                nc.tensor.matmul(out=gap[:], lhsT=minus_ident[:], rhs=x_tiles[j][:, b, cols], start=False, stop=True)
+                nc.tensor.matmul(
+                    out=gap[:], lhsT=ident_bf16[:], rhs=pred_tiles[b, side][:, row_cols], start=True, stop=False
+                )
+                nc.tensor.matmul(
+                    out=gap[:], lhsT=minus_ident[:], rhs=x_tiles[b, side][:, row_cols], start=False, stop=True
+                )
                 nc.scalar.copy(out=work[j][:, b, cols], in_=gap[:])
 
         for k in range(HALVES + LAG):
             if k < HALVES:
                 j, b, first = place(k)
-                som_words, inh_words, rneg = slabs[j]
+                som_words, inh_words = weight_tiles[j]
                 batch_cols = slice(b * P, (b + 1) * P)
-                side = j // (STEPS // 2)
                 for c in range(HALF // BANK):
                     cols = slice(first + c * BANK, first + (c + 1) * BANK)
-                    plane_first = (j % (STEPS // 2)) * WIDE + first + c * BANK
-                    plane_cols = slice(plane_first, plane_first + BANK)
                     inhibition = sum2_pool.tile([P, BANK], F32, name="inhibition")
                     nc.tensor.matmul_mx(
                         out=inhibition[:],
                         lhsT=som_codes[:, batch_cols].bitcast(FP8X4),
                         lhsT_scale=som_plane[:, batch_cols],
                         rhs=som_words[:, cols].bitcast(FP8X4),
-                        rhs_scale=out_planes[ROWS * (2 + side) : P, plane_cols],
+                        rhs_scale=som_planes[ROWS * j : P, cols],
                         start=True,
                         stop=False,
                     )
@@ -260,7 +293,7 @@ def tile_pecircuits_pb_k_kernel(
                         lhsT=pv_codes[:, batch_cols].bitcast(FP8X4),
                         lhsT_scale=pv_plane[:, batch_cols],
                         rhs=inh_words[:, cols].bitcast(FP8X4),
-                        rhs_scale=out_planes[ROWS * side : P, plane_cols],
+                        rhs_scale=inh_planes[ROWS * j : P, cols],
                         start=False,
                         stop=True,
                     )
@@ -275,19 +308,16 @@ def tile_pecircuits_pb_k_kernel(
                 )
             if k >= LAG:
                 j, b, first = place(k - LAG)
-                rneg = slabs[j][2]
+                side, slab_cols = side_cols(j)
                 half_cols = slice(first, first + HALF)
+                row_first = slab_cols.start + first
                 nc.vector.scalar_tensor_tensor(
                     out=work[j][:, b, half_cols],
-                    in0=rneg[:, b, half_cols],
+                    in0=rneg_tiles[b, side][:, row_first : row_first + HALF],
                     scalar=1.0 - ALPHA,
                     in1=work[j][:, b, half_cols],
                     op0=ALU.mult,
                     op1=ALU.add,
                 )
-                nc.sync.dma_start(
-                    out=out_view[:, b, j * WIDE + first : j * WIDE + first + HALF],
-                    in_=work[j][:, b, half_cols],
-                )
-                if (k - LAG) % HALVES_PER_SLAB == HALVES_PER_SLAB - 1 and j + AHEAD < STEPS:
-                    load_slab(j + AHEAD)
+                if first + HALF == WIDE:
+                    nc.sync.dma_start(out=out_view[:, b, j * WIDE : (j + 1) * WIDE], in_=work[j][:, b, :])

@@ -110,14 +110,16 @@ def tile_pecircuits_pb_k_kernel(
             rows = ring.tile([P, ROW], BF16, name="rows", tag="ring", align_bytes=64)
             load_rows(tiles, b, side, dram, rows)
 
-        def load_ff(s):
+        def load_ff(s, parts=1):
             ff_tiles[s] = ring.tile([P, GROUPS, HIDDEN], U32, name="ff_words", tag="ring", align_bytes=64)
-            nc.sync.dma_start(
-                out=ff_tiles[s][:].bitcast(I32),
-                in_=W_pv1_ff_words[s * GROUPS : (s + 1) * GROUPS]
-                .rearrange("g p n t -> p g (n t)")
-                .bitcast(I32),
-            )
+            size = GROUPS // parts
+            for first in range(0, GROUPS, size):
+                nc.sync.dma_start(
+                    out=ff_tiles[s][:, first : first + size, :].bitcast(I32),
+                    in_=W_pv1_ff_words[s * GROUPS + first : s * GROUPS + first + size]
+                    .rearrange("g p n t -> p g (n t)")
+                    .bitcast(I32),
+                )
 
         def load_ff_scales(s):
             for quad in range(QUADS):
@@ -137,14 +139,17 @@ def tile_pecircuits_pb_k_kernel(
                     .bitcast(I32),
                 )
 
-        def load_weights(j):
-            byte_cols = slice(j * WIDE * PACK, (j + 1) * WIDE * PACK)
-            pair = []
-            for view in (som_view, inh_view):
-                words = ring.tile([P, WIDE], U32, name="words", tag="ring", align_bytes=64)
-                nc.sync.dma_start(out=words[:].bitcast(I32), in_=view[:, byte_cols].bitcast(I32))
-                pair.append(words)
-            weight_tiles[j] = pair
+        def load_weights(j, parts=1):
+            som_words = ring.tile([P, WIDE], U32, name="som_words", tag="ring", align_bytes=64)
+            inh_words = ring.tile([P, WIDE], U32, name="inh_words", tag="ring", align_bytes=64)
+            weight_tiles[j] = (som_words, inh_words)
+            size = WIDE // parts
+            for first in range(0, WIDE, size):
+                byte_cols = slice((j * WIDE + first) * PACK, (j * WIDE + first + size) * PACK)
+                for words, view in zip(weight_tiles[j], (som_view, inh_view)):
+                    nc.sync.dma_start(
+                        out=words[:, first : first + size].bitcast(I32), in_=view[:, byte_cols].bitcast(I32)
+                    )
 
         work = [keep.tile([P, B_TILES, WIDE], F32, name="work%d" % s) for s in range(STEPS)]
 
@@ -152,12 +157,13 @@ def tile_pecircuits_pb_k_kernel(
             first = s * WIDE % ROW
             return s * WIDE // ROW, slice(first, first + WIDE)
 
-        def difference(s, b):
-            side, cols = side_cols(s)
+        def difference(s, b, cols):
+            side, slab_cols = side_cols(s)
+            row_cols = slice(slab_cols.start + cols.start, slab_cols.start + cols.stop)
             nc.vector.tensor_tensor(
-                out=work[s][:, b, :],
-                in0=pred_tiles[b, side][:, cols],
-                in1=x_tiles[b, side][:, cols],
+                out=work[s][:, b, cols],
+                in0=pred_tiles[b, side][:, row_cols],
+                in1=x_tiles[b, side][:, row_cols],
                 op=ALU.subtract,
             )
 
@@ -165,23 +171,21 @@ def tile_pecircuits_pb_k_kernel(
         load_ff_scales(0)
         ring_rows(x_tiles, 1, 0, x_batch)
         load_ff(0)
-        load_ff_scales(1)
-        load_ff(1)
         som_rows = keep.tile([P, B_TILES, HIDDEN], BF16, name="som_rows")
         nc.sync.dma_start(out=som_rows[:], in_=r_som.rearrange("(b p) k -> p b k", p=P))
-        ring_rows(pred_tiles, 0, 0, predicted)
-        load_ff_scales(2)
-        ring_rows(pred_tiles, 1, 0, predicted)
-        load_ff_scales(3)
+        load_ff_scales(1)
         for b in range(B_TILES):
             kept = keep.tile([P, ROW], BF16, name="x_kept%d" % b)
             load_rows(x_tiles, b, 1, x_batch, kept)
+            load_ff_scales(2 + b)
+        load_ff(1)
+        for b in range(B_TILES):
             load_out_scales(2 * b)
+            ring_rows(pred_tiles, b, 0, predicted)
+            load_out_scales(2 * b + 1)
         load_ff(2)
-        load_out_scales(1)
-        load_ff(3)
-        load_out_scales(3)
-        load_weights(0)
+        load_ff(3, parts=2)
+        load_weights(0, parts=2)
         for b in range(B_TILES):
             ring_rows(rneg_tiles, b, 0, r_neg_batch)
         load_weights(1)
@@ -192,34 +196,70 @@ def tile_pecircuits_pb_k_kernel(
         pv_codes = keep.tile([P, BATCH], U32, name="pv_codes", align_bytes=64)
         pv_plane = keep.tile([P, BATCH], U8, name="pv_plane", align_bytes=64)
 
-        for s in range(STEPS):
-            x_codes = []
-            x_planes = []
-            if s == 2:
-                rows = [som_rows[:, b, :] for b in range(B_TILES)]
-                quantise_group(nc, flip_pool, stage, ident_f32[:], rows, som_codes[:], som_plane[:])
+        x_quantised = {}
+
+        def quantise_slab(s):
             side, slab_cols = side_cols(s)
+            x_quantised[s] = []
             for i in range(GROUPS):
-                x_codes.append(stage.tile([P, BATCH], U32, name="x_codes", align_bytes=64))
-                x_planes.append(stage.tile([P, BATCH], U8, name="x_plane", align_bytes=64))
+                codes = stage.tile([P, BATCH], U32, name="x_codes", bufs=2 * GROUPS, align_bytes=64)
+                plane = stage.tile([P, BATCH], U8, name="x_plane", bufs=2 * GROUPS, align_bytes=64)
                 first = slab_cols.start + i * K_PASS
                 rows = [x_tiles[b, side][:, first : first + K_PASS] for b in range(B_TILES)]
-                quantise_group(nc, flip_pool, stage, ident_f32[:], rows, x_codes[i][:], x_planes[i][:])
-            for i in range(GROUPS):
+                quantise_group(nc, flip_pool, stage, ident_f32[:], rows, codes[:], plane[:])
+                x_quantised[s].append((codes, plane))
+
+        def multiply_slab(s):
+            for pair in range(0, GROUPS, 2):
                 for b in range(B_TILES):
                     batch_cols = slice(b * P, (b + 1) * P)
-                    nc.tensor.matmul_mx(
-                        out=hidden_sum[b][:],
-                        lhsT=x_codes[i][:, batch_cols].bitcast(FP8X4),
-                        lhsT_scale=x_planes[i][:, batch_cols],
-                        rhs=ff_tiles[s][:, i, :].bitcast(FP8X4),
-                        rhs_scale=ff_planes[ROWS * i : P, s, :],
-                        start=(s == 0 and i == 0),
-                        stop=(s == STEPS - 1 and i == GROUPS - 1),
-                    )
-            if s >= 1 and s - 1 < VECTOR_SLABS:
-                for b in range(B_TILES):
-                    difference(s - 1, b)
+                    for i in (pair, pair + 1):
+                        codes, plane = x_quantised[s][i]
+                        nc.tensor.matmul_mx(
+                            out=hidden_sum[b][:],
+                            lhsT=codes[:, batch_cols].bitcast(FP8X4),
+                            lhsT_scale=plane[:, batch_cols],
+                            rhs=ff_tiles[s][:, i, :].bitcast(FP8X4),
+                            rhs_scale=ff_planes[ROWS * i : P, s, :],
+                            start=(s == 0 and i == 0),
+                            stop=(s == STEPS - 1 and i == GROUPS - 1),
+                        )
+
+        quantise_slab(0)
+        for s in range(STEPS):
+            if s + 1 < STEPS:
+                quantise_slab(s + 1)
+            if s == 0:
+                som_row_tiles = [som_rows[:, b, :] for b in range(B_TILES)]
+                quantise_group(nc, flip_pool, stage, ident_f32[:], som_row_tiles, som_codes[:], som_plane[:])
+            if s + 1 == STEPS - 1:
+                for s_pred, b in ((0, 0), (1, 0), (0, 1)):
+                    difference(s_pred, b, slice(0, WIDE))
+            multiply_slab(s)
+
+        rates = [keep.tile([P, PACK, P], BF16, name="rates%d" % b) for b in range(B_TILES)]
+        by_word = [hidden_sum[b][:].rearrange("r (p t) -> r t p", t=PACK) for b in range(B_TILES)]
+        nc.scalar.activation(out=rates[0][:], in_=by_word[0], func=ACT.Relu)
+        nc.vector.tensor_scalar_max(out=rates[1][:], in0=by_word[1], scalar1=0.0)
+        turned = []
+        for b in range(B_TILES):
+            turned.append(flip_pool.tile([P, PACK, P], BF16, name="turned", tag="flip"))
+            for t in range(PACK):
+                nc.tensor.transpose(turned[b][:, t, :], rates[b][:, t, :], ident_bf16[:])
+        pv_grouped = [keep.tile([P, P, PACK], BF16, name="pv_grouped%d" % b, align_bytes=64) for b in range(B_TILES)]
+        nc.scalar.copy(out=pv_grouped[0][:], in_=turned[0][:].rearrange("p t r -> p r t"))
+        for b in range(B_TILES):
+            if b == 1:
+                nc.vector.tensor_copy(out=pv_grouped[1][:], in_=turned[1][:].rearrange("p t r -> p r t"))
+            batch_cols = slice(b * P, (b + 1) * P)
+            nc.vector.quantize_mx(
+                out=pv_codes[:, batch_cols].bitcast(FP8X4),
+                scales=pv_plane[:, batch_cols],
+                in_=pv_grouped[b][:].rearrange("p r t -> p (r t)"),
+            )
+
+        for first in range(0, WIDE, HALF):
+            difference(1, 1, slice(first, first + HALF))
 
         for b in range(B_TILES):
             ring_rows(pred_tiles, b, 1, predicted)
@@ -228,32 +268,18 @@ def tile_pecircuits_pb_k_kernel(
             ring_rows(rneg_tiles, b, 1, r_neg_batch)
         load_weights(3)
 
-        rates = [keep.tile([P, PACK, P], BF16, name="rates%d" % b) for b in range(B_TILES)]
-        for b in range(B_TILES):
-            nc.scalar.activation(
-                out=rates[b][:],
-                in_=hidden_sum[b][:].rearrange("r (p t) -> r t p", t=PACK),
-                func=ACT.Relu,
-            )
-        turned = []
-        for b in range(B_TILES):
-            turned.append(flip_pool.tile([P, PACK, P], BF16, name="turned", tag="flip"))
-            for t in range(PACK):
-                nc.tensor.transpose(turned[b][:, t, :], rates[b][:, t, :], ident_bf16[:])
-        for b in range(B_TILES):
-            batch_cols = slice(b * P, (b + 1) * P)
-            pv_grouped = keep.tile([P, P, PACK], BF16, name="pv_grouped%d" % b, align_bytes=64)
-            nc.scalar.copy(out=pv_grouped[:], in_=turned[b][:].rearrange("p t r -> p r t"))
-            nc.vector.quantize_mx(
-                out=pv_codes[:, batch_cols].bitcast(FP8X4),
-                scales=pv_plane[:, batch_cols],
-                in_=pv_grouped[:].rearrange("p r t -> p (r t)"),
-            )
-
         def place(k):
             j, rest = divmod(k, HALVES_PER_SLAB)
             b, h = divmod(rest, PIECES)
             return j, b, h * HALF
+
+        def grain(k):
+            return BANK if k == HALVES - 1 else HALF
+
+        def store(j, b, cols):
+            nc.sync.dma_start(
+                out=out_view[:, b, j * WIDE + cols.start : j * WIDE + cols.stop], in_=work[j][:, b, cols]
+            )
 
         def difference_by_tensor(k):
             j, b, first = place(k)
@@ -302,22 +328,23 @@ def tile_pecircuits_pb_k_kernel(
                     )
                 if VECTOR_SLABS * HALVES_PER_SLAB <= k + HALVES_PER_SLAB < HALVES:
                     difference_by_tensor(k + HALVES_PER_SLAB)
-                half_cols = slice(first, first + HALF)
-                nc.scalar.activation(
-                    out=work[j][:, b, half_cols], in_=work[j][:, b, half_cols], func=ACT.Relu, scale=ALPHA
-                )
+                for start in range(first, first + HALF, grain(k)):
+                    cols = slice(start, start + grain(k))
+                    nc.scalar.activation(out=work[j][:, b, cols], in_=work[j][:, b, cols], func=ACT.Relu, scale=ALPHA)
             if k >= LAG:
                 j, b, first = place(k - LAG)
                 side, slab_cols = side_cols(j)
-                half_cols = slice(first, first + HALF)
-                row_first = slab_cols.start + first
-                nc.vector.scalar_tensor_tensor(
-                    out=work[j][:, b, half_cols],
-                    in0=rneg_tiles[b, side][:, row_first : row_first + HALF],
-                    scalar=1.0 - ALPHA,
-                    in1=work[j][:, b, half_cols],
-                    op0=ALU.mult,
-                    op1=ALU.add,
-                )
-                if first + HALF == WIDE:
-                    nc.sync.dma_start(out=out_view[:, b, j * WIDE : (j + 1) * WIDE], in_=work[j][:, b, :])
+                for start in range(first, first + HALF, grain(k - LAG)):
+                    cols = slice(start, start + grain(k - LAG))
+                    nc.vector.scalar_tensor_tensor(
+                        out=work[j][:, b, cols],
+                        in0=rneg_tiles[b, side][:, slab_cols.start + cols.start : slab_cols.start + cols.stop],
+                        scalar=1.0 - ALPHA,
+                        in1=work[j][:, b, cols],
+                        op0=ALU.mult,
+                        op1=ALU.add,
+                    )
+                    if k - LAG >= HALVES - PIECES:
+                        store(j, b, cols)
+                if k - LAG < HALVES - PIECES and first + HALF == WIDE:
+                    store(j, b, slice(0, WIDE))

@@ -34,7 +34,7 @@ HALVES_PER_SLAB = B_TILES * WIDE // HALF
 PIECES = WIDE // HALF
 RING = 14
 LAG = 2
-VECTOR_SLABS = 2
+VECTOR_HALVES = 7
 QUADS = 4
 ROWS = 4
 
@@ -102,18 +102,25 @@ def tile_pecircuits_pb_k_kernel(
         ff_tiles = {}
         weight_tiles = {}
 
-        def load_rows(tiles, b, side, dram, tile):
-            tiles[b, side] = tile
-            nc.sync.dma_start(out=tile[:], in_=dram[b * P : (b + 1) * P, side * ROW : (side + 1) * ROW])
+        def load_rows(tiles, b, side, dram, first=0, last=ROW):
+            nc.sync.dma_start(
+                out=tiles[b, side][:, first:last],
+                in_=dram[b * P : (b + 1) * P, side * ROW + first : side * ROW + last],
+            )
 
-        def ring_rows(tiles, b, side, dram):
-            rows = ring.tile([P, ROW], BF16, name="rows", tag="ring", align_bytes=64)
-            load_rows(tiles, b, side, dram, rows)
+        def ring_rows(tiles, b, side):
+            tiles[b, side] = ring.tile([P, ROW], BF16, name="rows", tag="ring", align_bytes=64)
 
-        def load_ff(s, parts=1):
+        def ring_ff(s):
             ff_tiles[s] = ring.tile([P, GROUPS, HIDDEN], U32, name="ff_words", tag="ring", align_bytes=64)
-            size = GROUPS // parts
-            for first in range(0, GROUPS, size):
+
+        def ring_weights(j):
+            som_words = ring.tile([P, WIDE], U32, name="som_words", tag="ring", align_bytes=64)
+            inh_words = ring.tile([P, WIDE], U32, name="inh_words", tag="ring", align_bytes=64)
+            weight_tiles[j] = (som_words, inh_words)
+
+        def load_ff(s, cuts=(0, GROUPS)):
+            for first, size in [(a, b - a) for a, b in zip(cuts, cuts[1:])]:
                 nc.sync.dma_start(
                     out=ff_tiles[s][:, first : first + size, :].bitcast(I32),
                     in_=W_pv1_ff_words[s * GROUPS + first : s * GROUPS + first + size]
@@ -140,9 +147,6 @@ def tile_pecircuits_pb_k_kernel(
                 )
 
         def load_weights(j, parts=1):
-            som_words = ring.tile([P, WIDE], U32, name="som_words", tag="ring", align_bytes=64)
-            inh_words = ring.tile([P, WIDE], U32, name="inh_words", tag="ring", align_bytes=64)
-            weight_tiles[j] = (som_words, inh_words)
             size = WIDE // parts
             for first in range(0, WIDE, size):
                 byte_cols = slice((j * WIDE + first) * PACK, (j * WIDE + first + size) * PACK)
@@ -167,27 +171,44 @@ def tile_pecircuits_pb_k_kernel(
                 op=ALU.subtract,
             )
 
-        ring_rows(x_tiles, 0, 0, x_batch)
+        ring_rows(x_tiles, 0, 0)
+        ring_ff(0)
+        ring_rows(pred_tiles, 0, 0)
+        for s in range(1, STEPS):
+            ring_ff(s)
+        ring_rows(x_tiles, 1, 0)
+        ring_rows(pred_tiles, 1, 0)
+        ring_weights(0)
+        for b in range(B_TILES):
+            ring_rows(rneg_tiles, b, 0)
+        ring_weights(1)
+        for b in range(B_TILES):
+            x_tiles[b, 1] = keep.tile([P, ROW], BF16, name="x_kept%d" % b)
+
+        early = VECTOR_HALVES * HALF - ROW
+        load_rows(x_tiles, 0, 0, x_batch)
         load_ff_scales(0)
-        ring_rows(x_tiles, 1, 0, x_batch)
+        load_rows(x_tiles, 1, 0, x_batch)
         load_ff(0)
         som_rows = keep.tile([P, B_TILES, HIDDEN], BF16, name="som_rows")
         nc.sync.dma_start(out=som_rows[:], in_=r_som.rearrange("(b p) k -> p b k", p=P))
         load_ff_scales(1)
         for b in range(B_TILES):
-            kept = keep.tile([P, ROW], BF16, name="x_kept%d" % b)
-            load_rows(x_tiles, b, 1, x_batch, kept)
+            load_rows(x_tiles, b, 1, x_batch)
             load_ff_scales(2 + b)
+        load_rows(pred_tiles, 0, 0, predicted)
+        load_out_scales(0)
         load_ff(1)
-        for b in range(B_TILES):
-            load_out_scales(2 * b)
-            ring_rows(pred_tiles, b, 0, predicted)
-            load_out_scales(2 * b + 1)
+        load_out_scales(1)
+        load_rows(pred_tiles, 1, 0, predicted, last=early)
+        load_out_scales(2)
         load_ff(2)
-        load_ff(3, parts=2)
+        load_out_scales(3)
+        load_ff(3, cuts=(0, GROUPS - 1, GROUPS))
         load_weights(0, parts=2)
-        for b in range(B_TILES):
-            ring_rows(rneg_tiles, b, 0, r_neg_batch)
+        load_rows(rneg_tiles, 0, 0, r_neg_batch)
+        load_rows(pred_tiles, 1, 0, predicted, first=early)
+        load_rows(rneg_tiles, 1, 0, r_neg_batch)
         load_weights(1)
 
         hidden_sum = [sum1_pool.tile([P, HIDDEN], F32, name="hidden_sum%d" % b) for b in range(B_TILES)]
@@ -202,39 +223,39 @@ def tile_pecircuits_pb_k_kernel(
             side, slab_cols = side_cols(s)
             x_quantised[s] = []
             for i in range(GROUPS):
-                codes = stage.tile([P, BATCH], U32, name="x_codes", bufs=2 * GROUPS, align_bytes=64)
-                plane = stage.tile([P, BATCH], U8, name="x_plane", bufs=2 * GROUPS, align_bytes=64)
+                codes = stage.tile([P, BATCH], U32, name="x_codes", bufs=3 * GROUPS, align_bytes=64)
+                plane = stage.tile([P, BATCH], U8, name="x_plane", bufs=3 * GROUPS, align_bytes=64)
                 first = slab_cols.start + i * K_PASS
                 rows = [x_tiles[b, side][:, first : first + K_PASS] for b in range(B_TILES)]
                 quantise_group(nc, flip_pool, stage, ident_f32[:], rows, codes[:], plane[:])
                 x_quantised[s].append((codes, plane))
 
         def multiply_slab(s):
-            for pair in range(0, GROUPS, 2):
+            for i in range(GROUPS):
+                codes, plane = x_quantised[s][i]
                 for b in range(B_TILES):
                     batch_cols = slice(b * P, (b + 1) * P)
-                    for i in (pair, pair + 1):
-                        codes, plane = x_quantised[s][i]
-                        nc.tensor.matmul_mx(
-                            out=hidden_sum[b][:],
-                            lhsT=codes[:, batch_cols].bitcast(FP8X4),
-                            lhsT_scale=plane[:, batch_cols],
-                            rhs=ff_tiles[s][:, i, :].bitcast(FP8X4),
-                            rhs_scale=ff_planes[ROWS * i : P, s, :],
-                            start=(s == 0 and i == 0),
-                            stop=(s == STEPS - 1 and i == GROUPS - 1),
-                        )
+                    nc.tensor.matmul_mx(
+                        out=hidden_sum[b][:],
+                        lhsT=codes[:, batch_cols].bitcast(FP8X4),
+                        lhsT_scale=plane[:, batch_cols],
+                        rhs=ff_tiles[s][:, i, :].bitcast(FP8X4),
+                        rhs_scale=ff_planes[ROWS * i : P, s, :],
+                        start=(s == 0 and i == 0),
+                        stop=(s == STEPS - 1 and i == GROUPS - 1),
+                    )
 
         quantise_slab(0)
-        for s in range(STEPS):
-            if s + 1 < STEPS:
-                quantise_slab(s + 1)
-            if s == 0:
-                som_row_tiles = [som_rows[:, b, :] for b in range(B_TILES)]
-                quantise_group(nc, flip_pool, stage, ident_f32[:], som_row_tiles, som_codes[:], som_plane[:])
-            if s + 1 == STEPS - 1:
-                for s_pred, b in ((0, 0), (1, 0), (0, 1)):
-                    difference(s_pred, b, slice(0, WIDE))
+        quantise_slab(1)
+        multiply_slab(0)
+        som_row_tiles = [som_rows[:, b, :] for b in range(B_TILES)]
+        quantise_group(nc, flip_pool, stage, ident_f32[:], som_row_tiles, som_codes[:], som_plane[:])
+        quantise_slab(2)
+        quantise_slab(3)
+        for slab, b in ((0, 0), (1, 0), (0, 1)):
+            difference(slab, b, slice(0, WIDE))
+        difference(1, 1, slice(0, early - WIDE))
+        for s in range(1, STEPS):
             multiply_slab(s)
 
         rates = [keep.tile([P, PACK, P], BF16, name="rates%d" % b) for b in range(B_TILES)]
@@ -258,15 +279,14 @@ def tile_pecircuits_pb_k_kernel(
                 in_=pv_grouped[b][:].rearrange("p r t -> p (r t)"),
             )
 
-        for first in range(0, WIDE, HALF):
-            difference(1, 1, slice(first, first + HALF))
-
         for b in range(B_TILES):
-            ring_rows(pred_tiles, b, 1, predicted)
+            ring_rows(pred_tiles, b, 1)
+            load_rows(pred_tiles, b, 1, predicted)
+        ring_weights(2)
         load_weights(2)
         for b in range(B_TILES):
-            ring_rows(rneg_tiles, b, 1, r_neg_batch)
-        load_weights(3)
+            ring_rows(rneg_tiles, b, 1)
+            load_rows(rneg_tiles, b, 1, r_neg_batch)
 
         def place(k):
             j, rest = divmod(k, HALVES_PER_SLAB)
@@ -326,8 +346,11 @@ def tile_pecircuits_pb_k_kernel(
                     nc.vector.tensor_tensor(
                         out=work[j][:, b, cols], in0=work[j][:, b, cols], in1=inhibition[:], op=ALU.subtract
                     )
-                if VECTOR_SLABS * HALVES_PER_SLAB <= k + HALVES_PER_SLAB < HALVES:
+                if VECTOR_HALVES <= k + HALVES_PER_SLAB < HALVES:
                     difference_by_tensor(k + HALVES_PER_SLAB)
+                if k + HALVES_PER_SLAB == VECTOR_HALVES:
+                    ring_weights(STEPS - 1)
+                    load_weights(STEPS - 1)
                 for start in range(first, first + HALF, grain(k)):
                     cols = slice(start, start + grain(k))
                     nc.scalar.activation(out=work[j][:, b, cols], in_=work[j][:, b, cols], func=ACT.Relu, scale=ALPHA)

@@ -27,12 +27,11 @@ WIDE = 2048
 STEPS = D // WIDE
 GROUPS = WIDE // K_PASS
 ROW = 2 * WIDE
-SIDES = D // ROW
 HALF = 2 * BANK
 HALVES = B_TILES * D // HALF
 HALVES_PER_SLAB = B_TILES * WIDE // HALF
 PIECES = WIDE // HALF
-RING = 14
+RING = 12
 LAG = 2
 VECTOR_HALVES = 7
 QUADS = 4
@@ -41,16 +40,19 @@ ROWS = 4
 FLOPS = 2 * BATCH * D * HIDDEN * 3
 
 
-def quantise_group(nc, flip_pool, stage, ident_f32, rows, codes, plane):
-    flipped = flip_pool.tile([P, 2, BATCH], F32, name="flipped", tag="flip")
-    for b in range(B_TILES):
-        words = rows[b].bitcast(F32)
+def quantise_pair(nc, flip_pool, stage, ident_f32, pair, codes, plane):
+    flipped = flip_pool.tile([P, 2, 2, P], F32, name="flipped", tag="flip")
+    for i, rows in enumerate(pair):
+        words = rows.bitcast(F32)
         for u in range(2):
-            nc.tensor.transpose(flipped[:, u, b * P : (b + 1) * P], words[:, u : K_PASS // 2 : 2], ident_f32)
-    grouped = stage.tile([P, BATCH, PACK], BF16, name="grouped", align_bytes=64)
-    nc.scalar.copy(out=grouped[:].bitcast(F32), in_=flipped[:].rearrange("p u c -> p c u"))
+            nc.tensor.transpose(flipped[:, i, u, :], words[:, u : K_PASS // 2 : 2], ident_f32)
+    grouped = stage.tile([P, 2, P, PACK], BF16, name="grouped", align_bytes=64)
+    nc.scalar.copy(
+        out=grouped[:].rearrange("p i r t -> p (i r t)").bitcast(F32).rearrange("p (i r u) -> p i r u", i=2, u=2),
+        in_=flipped[:].rearrange("p i u r -> p i r u"),
+    )
     nc.vector.quantize_mx(
-        out=codes.bitcast(FP8X4), scales=plane, in_=grouped[:].rearrange("p c t -> p (c t)")
+        out=codes.bitcast(FP8X4), scales=plane, in_=grouped[:].rearrange("p i r t -> p (i r t)")
     )
 
 
@@ -69,7 +71,6 @@ def tile_pecircuits_pb_k_kernel(
     out,
 ):
     nc = tc.nc
-    out_view = out.rearrange("(b p) k -> p b k", p=P)
     inh_view = W_inh_pe_neg_words[0].rearrange("p n t -> p (n t)")
     som_view = W_som_dend_words[0].rearrange("p n t -> p (n t)")
 
@@ -77,7 +78,7 @@ def tile_pecircuits_pb_k_kernel(
         ctx.enter_context(tc.manual_schedule())
         keep = ctx.enter_context(tc.tile_pool(name="keep", bufs=1))
         ring = ctx.enter_context(tc.tile_pool(name="ring", bufs=RING))
-        stage = ctx.enter_context(tc.tile_pool(name="stage", bufs=GROUPS))
+        stage = ctx.enter_context(tc.tile_pool(name="stage", bufs=3))
         sum1_pool = ctx.enter_context(tc.psum_pool(name="sum1_pool", bufs=1))
         flip_pool = ctx.enter_context(tc.psum_pool(name="flip_pool", bufs=3))
         sum2_pool = ctx.enter_context(tc.psum_pool(name="sum2_pool", bufs=3))
@@ -101,6 +102,10 @@ def tile_pecircuits_pb_k_kernel(
         rneg_tiles = {}
         ff_tiles = {}
         weight_tiles = {}
+
+        def load_x(b):
+            x_tiles[b] = keep.tile([P, D], BF16, name="x_rows%d" % b)
+            nc.sync.dma_start(out=x_tiles[b][:], in_=x_batch[b * P : (b + 1) * P, :])
 
         def load_rows(tiles, b, side, dram, first=0, last=ROW):
             nc.sync.dma_start(
@@ -155,54 +160,43 @@ def tile_pecircuits_pb_k_kernel(
                         out=words[:, first : first + size].bitcast(I32), in_=view[:, byte_cols].bitcast(I32)
                     )
 
-        work = [keep.tile([P, B_TILES, WIDE], F32, name="work%d" % s) for s in range(STEPS)]
+        work = [keep.tile([P, D], F32, name="work%d" % b) for b in range(B_TILES)]
 
-        def side_cols(s):
-            first = s * WIDE % ROW
-            return s * WIDE // ROW, slice(first, first + WIDE)
-
-        def difference(s, b, cols):
-            side, slab_cols = side_cols(s)
-            row_cols = slice(slab_cols.start + cols.start, slab_cols.start + cols.stop)
+        def difference(b, first, last):
             nc.vector.tensor_tensor(
-                out=work[s][:, b, cols],
-                in0=pred_tiles[b, side][:, row_cols],
-                in1=x_tiles[b, side][:, row_cols],
+                out=work[b][:, first:last],
+                in0=pred_tiles[b, 0][:, first:last],
+                in1=x_tiles[b][:, first:last],
                 op=ALU.subtract,
             )
 
-        ring_rows(x_tiles, 0, 0)
         ring_ff(0)
         ring_rows(pred_tiles, 0, 0)
         for s in range(1, STEPS):
             ring_ff(s)
-        ring_rows(x_tiles, 1, 0)
         ring_rows(pred_tiles, 1, 0)
         ring_weights(0)
         for b in range(B_TILES):
             ring_rows(rneg_tiles, b, 0)
         ring_weights(1)
-        for b in range(B_TILES):
-            x_tiles[b, 1] = keep.tile([P, ROW], BF16, name="x_kept%d" % b)
 
         early = VECTOR_HALVES * HALF - ROW
-        load_rows(x_tiles, 0, 0, x_batch)
+        load_x(0)
         load_ff_scales(0)
-        load_rows(x_tiles, 1, 0, x_batch)
+        load_x(1)
         load_ff(0)
         som_rows = keep.tile([P, B_TILES, HIDDEN], BF16, name="som_rows")
         nc.sync.dma_start(out=som_rows[:], in_=r_som.rearrange("(b p) k -> p b k", p=P))
         load_ff_scales(1)
-        for b in range(B_TILES):
-            load_rows(x_tiles, b, 1, x_batch)
-            load_ff_scales(2 + b)
         load_rows(pred_tiles, 0, 0, predicted)
-        load_out_scales(0)
+        load_ff_scales(2)
         load_ff(1)
-        load_out_scales(1)
+        load_ff_scales(3)
         load_rows(pred_tiles, 1, 0, predicted, last=early)
-        load_out_scales(2)
+        load_out_scales(0)
+        load_out_scales(1)
         load_ff(2)
+        load_out_scales(2)
         load_out_scales(3)
         load_ff(3, cuts=(0, GROUPS - 1, GROUPS))
         load_weights(0, parts=2)
@@ -219,43 +213,39 @@ def tile_pecircuits_pb_k_kernel(
 
         x_quantised = {}
 
-        def quantise_slab(s):
-            side, slab_cols = side_cols(s)
-            x_quantised[s] = []
-            for i in range(GROUPS):
-                codes = stage.tile([P, BATCH], U32, name="x_codes", bufs=3 * GROUPS, align_bytes=64)
-                plane = stage.tile([P, BATCH], U8, name="x_plane", bufs=3 * GROUPS, align_bytes=64)
-                first = slab_cols.start + i * K_PASS
-                rows = [x_tiles[b, side][:, first : first + K_PASS] for b in range(B_TILES)]
-                quantise_group(nc, flip_pool, stage, ident_f32[:], rows, codes[:], plane[:])
-                x_quantised[s].append((codes, plane))
+        def quantise_x(b):
+            for pair in range(0, D // K_PASS, 2):
+                codes = stage.tile([P, 2 * P], U32, name="x_codes", bufs=D // K_PASS, align_bytes=64)
+                plane = stage.tile([P, 2 * P], U8, name="x_plane", bufs=D // K_PASS, align_bytes=64)
+                sets = [x_tiles[b][:, g * K_PASS : (g + 1) * K_PASS] for g in (pair, pair + 1)]
+                quantise_pair(nc, flip_pool, stage, ident_f32[:], sets, codes[:], plane[:])
+                x_quantised[b, pair // 2] = (codes, plane)
 
         def multiply_slab(s):
             for i in range(GROUPS):
-                codes, plane = x_quantised[s][i]
+                g = s * GROUPS + i
+                code_cols = slice(g % 2 * P, (g % 2 + 1) * P)
                 for b in range(B_TILES):
-                    batch_cols = slice(b * P, (b + 1) * P)
+                    codes, plane = x_quantised[b, g // 2]
                     nc.tensor.matmul_mx(
                         out=hidden_sum[b][:],
-                        lhsT=codes[:, batch_cols].bitcast(FP8X4),
-                        lhsT_scale=plane[:, batch_cols],
+                        lhsT=codes[:, code_cols].bitcast(FP8X4),
+                        lhsT_scale=plane[:, code_cols],
                         rhs=ff_tiles[s][:, i, :].bitcast(FP8X4),
                         rhs_scale=ff_planes[ROWS * i : P, s, :],
-                        start=(s == 0 and i == 0),
-                        stop=(s == STEPS - 1 and i == GROUPS - 1),
+                        start=(g == 0),
+                        stop=(g == D // K_PASS - 1),
                     )
 
-        quantise_slab(0)
-        quantise_slab(1)
-        multiply_slab(0)
-        som_row_tiles = [som_rows[:, b, :] for b in range(B_TILES)]
-        quantise_group(nc, flip_pool, stage, ident_f32[:], som_row_tiles, som_codes[:], som_plane[:])
-        quantise_slab(2)
-        quantise_slab(3)
-        for slab, b in ((0, 0), (1, 0), (0, 1)):
-            difference(slab, b, slice(0, WIDE))
-        difference(1, 1, slice(0, early - WIDE))
-        for s in range(1, STEPS):
+        for b in range(B_TILES):
+            quantise_x(b)
+        som_sets = [som_rows[:, b, :] for b in range(B_TILES)]
+        quantise_pair(nc, flip_pool, stage, ident_f32[:], som_sets, som_codes[:], som_plane[:])
+        difference(0, 0, WIDE)
+        difference(0, WIDE, ROW)
+        difference(1, 0, WIDE)
+        difference(1, WIDE, early)
+        for s in range(STEPS):
             multiply_slab(s)
 
         rates = [keep.tile([P, PACK, P], BF16, name="rates%d" % b) for b in range(B_TILES)]
@@ -284,46 +274,44 @@ def tile_pecircuits_pb_k_kernel(
             load_rows(pred_tiles, b, 1, predicted)
         ring_weights(2)
         load_weights(2)
-        for b in range(B_TILES):
-            ring_rows(rneg_tiles, b, 1)
-            load_rows(rneg_tiles, b, 1, r_neg_batch)
+        ring_rows(rneg_tiles, 0, 1)
+        load_rows(rneg_tiles, 0, 1, r_neg_batch)
 
         def place(k):
             j, rest = divmod(k, HALVES_PER_SLAB)
             b, h = divmod(rest, PIECES)
-            return j, b, h * HALF
+            return j, b, j * WIDE + h * HALF
 
         def grain(k):
             return BANK if k == HALVES - 1 else HALF
 
-        def store(j, b, cols):
-            nc.sync.dma_start(
-                out=out_view[:, b, j * WIDE + cols.start : j * WIDE + cols.stop], in_=work[j][:, b, cols]
-            )
+        def store(b, first, last):
+            nc.sync.dma_start(out=out[b * P : (b + 1) * P, first:last], in_=work[b][:, first:last])
 
         def difference_by_tensor(k):
             j, b, first = place(k)
-            side, slab_cols = side_cols(j)
-            for c in range(HALF // BANK):
-                start = first + c * BANK
-                cols = slice(start, start + BANK)
-                row_cols = slice(slab_cols.start + start, slab_cols.start + start + BANK)
+            for start in range(first, first + HALF, BANK):
+                side, row_first = divmod(start, ROW)
                 gap = flip_pool.tile([P, BANK], F32, name="gap", tag="flip")
                 nc.tensor.matmul(
-                    out=gap[:], lhsT=ident_bf16[:], rhs=pred_tiles[b, side][:, row_cols], start=True, stop=False
+                    out=gap[:],
+                    lhsT=ident_bf16[:],
+                    rhs=pred_tiles[b, side][:, row_first : row_first + BANK],
+                    start=True,
+                    stop=False,
                 )
                 nc.tensor.matmul(
-                    out=gap[:], lhsT=minus_ident[:], rhs=x_tiles[b, side][:, row_cols], start=False, stop=True
+                    out=gap[:], lhsT=minus_ident[:], rhs=x_tiles[b][:, start : start + BANK], start=False, stop=True
                 )
-                nc.scalar.copy(out=work[j][:, b, cols], in_=gap[:])
+                nc.scalar.copy(out=work[b][:, start : start + BANK], in_=gap[:])
 
         for k in range(HALVES + LAG):
             if k < HALVES:
                 j, b, first = place(k)
                 som_words, inh_words = weight_tiles[j]
                 batch_cols = slice(b * P, (b + 1) * P)
-                for c in range(HALF // BANK):
-                    cols = slice(first + c * BANK, first + (c + 1) * BANK)
+                for start in range(first, first + HALF, BANK):
+                    cols = slice(start - j * WIDE, start - j * WIDE + BANK)
                     inhibition = sum2_pool.tile([P, BANK], F32, name="inhibition")
                     nc.tensor.matmul_mx(
                         out=inhibition[:],
@@ -343,31 +331,37 @@ def tile_pecircuits_pb_k_kernel(
                         start=False,
                         stop=True,
                     )
-                    nc.vector.tensor_tensor(
-                        out=work[j][:, b, cols], in0=work[j][:, b, cols], in1=inhibition[:], op=ALU.subtract
-                    )
+                    part = work[b][:, start : start + BANK]
+                    nc.vector.tensor_tensor(out=part, in0=part, in1=inhibition[:], op=ALU.subtract)
                 if VECTOR_HALVES <= k + HALVES_PER_SLAB < HALVES:
                     difference_by_tensor(k + HALVES_PER_SLAB)
                 if k + HALVES_PER_SLAB == VECTOR_HALVES:
+                    ring_rows(rneg_tiles, 1, 1)
+                    load_rows(rneg_tiles, 1, 1, r_neg_batch)
                     ring_weights(STEPS - 1)
                     load_weights(STEPS - 1)
                 for start in range(first, first + HALF, grain(k)):
-                    cols = slice(start, start + grain(k))
-                    nc.scalar.activation(out=work[j][:, b, cols], in_=work[j][:, b, cols], func=ACT.Relu, scale=ALPHA)
+                    part = work[b][:, start : start + grain(k)]
+                    nc.scalar.activation(out=part, in_=part, func=ACT.Relu, scale=ALPHA)
             if k >= LAG:
-                j, b, first = place(k - LAG)
-                side, slab_cols = side_cols(j)
-                for start in range(first, first + HALF, grain(k - LAG)):
-                    cols = slice(start, start + grain(k - LAG))
+                done = k - LAG
+                j, b, first = place(done)
+                side = first // ROW
+                last = first + HALF
+                for start in range(first, last, grain(done)):
+                    part = work[b][:, start : start + grain(done)]
+                    row_first = start - side * ROW
                     nc.vector.scalar_tensor_tensor(
-                        out=work[j][:, b, cols],
-                        in0=rneg_tiles[b, side][:, slab_cols.start + cols.start : slab_cols.start + cols.stop],
+                        out=part,
+                        in0=rneg_tiles[b, side][:, row_first : row_first + grain(done)],
                         scalar=1.0 - ALPHA,
-                        in1=work[j][:, b, cols],
+                        in1=part,
                         op0=ALU.mult,
                         op1=ALU.add,
                     )
-                    if k - LAG >= HALVES - PIECES:
-                        store(j, b, cols)
-                if k - LAG < HALVES - PIECES and first + HALF == WIDE:
-                    store(j, b, slice(0, WIDE))
+                    if done >= HALVES - PIECES:
+                        store(b, start, start + grain(done))
+                if side == 0 and last == ROW:
+                    store(b, 0, last)
+                if side > 0 and last % WIDE == 0 and done < HALVES - PIECES:
+                    store(b, last - WIDE, last)

@@ -33,7 +33,7 @@ HALVES_PER_SLAB = B_TILES * WIDE // HALF
 PIECES = WIDE // HALF
 RING = 12
 LAG = 2
-VECTOR_HALVES = 7
+VECTOR_HALVES = 8
 QUADS = 4
 ROWS = 4
 
@@ -107,10 +107,9 @@ def tile_pecircuits_pb_k_kernel(
             x_tiles[b] = keep.tile([P, D], BF16, name="x_rows%d" % b)
             nc.sync.dma_start(out=x_tiles[b][:], in_=x_batch[b * P : (b + 1) * P, :])
 
-        def load_rows(tiles, b, side, dram, first=0, last=ROW):
+        def load_rows(tiles, b, side, dram):
             nc.sync.dma_start(
-                out=tiles[b, side][:, first:last],
-                in_=dram[b * P : (b + 1) * P, side * ROW + first : side * ROW + last],
+                out=tiles[b, side][:], in_=dram[b * P : (b + 1) * P, side * ROW : (side + 1) * ROW]
             )
 
         def ring_rows(tiles, b, side):
@@ -124,14 +123,11 @@ def tile_pecircuits_pb_k_kernel(
             inh_words = ring.tile([P, WIDE], U32, name="inh_words", tag="ring", align_bytes=64)
             weight_tiles[j] = (som_words, inh_words)
 
-        def load_ff(s, cuts=(0, GROUPS)):
-            for first, size in [(a, b - a) for a, b in zip(cuts, cuts[1:])]:
-                nc.sync.dma_start(
-                    out=ff_tiles[s][:, first : first + size, :].bitcast(I32),
-                    in_=W_pv1_ff_words[s * GROUPS + first : s * GROUPS + first + size]
-                    .rearrange("g p n t -> p g (n t)")
-                    .bitcast(I32),
-                )
+        def load_ff(s):
+            nc.sync.dma_start(
+                out=ff_tiles[s][:].bitcast(I32),
+                in_=W_pv1_ff_words[s * GROUPS : (s + 1) * GROUPS].rearrange("g p n t -> p g (n t)").bitcast(I32),
+            )
 
         def load_ff_scales(s):
             for quad in range(QUADS):
@@ -151,14 +147,10 @@ def tile_pecircuits_pb_k_kernel(
                     .bitcast(I32),
                 )
 
-        def load_weights(j, parts=1):
-            size = WIDE // parts
-            for first in range(0, WIDE, size):
-                byte_cols = slice((j * WIDE + first) * PACK, (j * WIDE + first + size) * PACK)
-                for words, view in zip(weight_tiles[j], (som_view, inh_view)):
-                    nc.sync.dma_start(
-                        out=words[:, first : first + size].bitcast(I32), in_=view[:, byte_cols].bitcast(I32)
-                    )
+        def load_weights(j):
+            byte_cols = slice(j * WIDE * PACK, (j + 1) * WIDE * PACK)
+            for words, view in zip(weight_tiles[j], (som_view, inh_view)):
+                nc.sync.dma_start(out=words[:].bitcast(I32), in_=view[:, byte_cols].bitcast(I32))
 
         work = [keep.tile([P, D], F32, name="work%d" % b) for b in range(B_TILES)]
 
@@ -180,7 +172,6 @@ def tile_pecircuits_pb_k_kernel(
             ring_rows(rneg_tiles, b, 0)
         ring_weights(1)
 
-        early = VECTOR_HALVES * HALF - ROW
         load_x(0)
         load_ff_scales(0)
         load_x(1)
@@ -192,16 +183,15 @@ def tile_pecircuits_pb_k_kernel(
         load_ff_scales(2)
         load_ff(1)
         load_ff_scales(3)
-        load_rows(pred_tiles, 1, 0, predicted, last=early)
+        load_rows(pred_tiles, 1, 0, predicted)
         load_out_scales(0)
         load_out_scales(1)
         load_ff(2)
         load_out_scales(2)
         load_out_scales(3)
-        load_ff(3, cuts=(0, GROUPS - 1, GROUPS))
-        load_weights(0, parts=2)
+        load_ff(3)
+        load_weights(0)
         load_rows(rneg_tiles, 0, 0, r_neg_batch)
-        load_rows(pred_tiles, 1, 0, predicted, first=early)
         load_rows(rneg_tiles, 1, 0, r_neg_batch)
         load_weights(1)
 
@@ -244,7 +234,7 @@ def tile_pecircuits_pb_k_kernel(
         difference(0, 0, WIDE)
         difference(0, WIDE, ROW)
         difference(1, 0, WIDE)
-        difference(1, WIDE, early)
+        difference(1, WIDE, ROW)
         for s in range(STEPS):
             multiply_slab(s)
 
@@ -281,9 +271,6 @@ def tile_pecircuits_pb_k_kernel(
             j, rest = divmod(k, HALVES_PER_SLAB)
             b, h = divmod(rest, PIECES)
             return j, b, j * WIDE + h * HALF
-
-        def grain(k):
-            return BANK if k == HALVES - 1 else HALF
 
         def store(b, first, last):
             nc.sync.dma_start(out=out[b * P : (b + 1) * P, first:last], in_=work[b][:, first:last])
@@ -335,33 +322,28 @@ def tile_pecircuits_pb_k_kernel(
                     nc.vector.tensor_tensor(out=part, in0=part, in1=inhibition[:], op=ALU.subtract)
                 if VECTOR_HALVES <= k + HALVES_PER_SLAB < HALVES:
                     difference_by_tensor(k + HALVES_PER_SLAB)
-                if k + HALVES_PER_SLAB == VECTOR_HALVES:
+                if k == HALVES_PER_SLAB - 1:
                     ring_rows(rneg_tiles, 1, 1)
                     load_rows(rneg_tiles, 1, 1, r_neg_batch)
                     ring_weights(STEPS - 1)
                     load_weights(STEPS - 1)
-                for start in range(first, first + HALF, grain(k)):
-                    part = work[b][:, start : start + grain(k)]
-                    nc.scalar.activation(out=part, in_=part, func=ACT.Relu, scale=ALPHA)
+                part = work[b][:, first : first + HALF]
+                nc.scalar.activation(out=part, in_=part, func=ACT.Relu, scale=ALPHA)
             if k >= LAG:
                 done = k - LAG
                 j, b, first = place(done)
                 side = first // ROW
                 last = first + HALF
-                for start in range(first, last, grain(done)):
-                    part = work[b][:, start : start + grain(done)]
-                    row_first = start - side * ROW
-                    nc.vector.scalar_tensor_tensor(
-                        out=part,
-                        in0=rneg_tiles[b, side][:, row_first : row_first + grain(done)],
-                        scalar=1.0 - ALPHA,
-                        in1=part,
-                        op0=ALU.mult,
-                        op1=ALU.add,
-                    )
-                    if done >= HALVES - PIECES:
-                        store(b, start, start + grain(done))
-                if side == 0 and last == ROW:
+                part = work[b][:, first:last]
+                nc.vector.scalar_tensor_tensor(
+                    out=part,
+                    in0=rneg_tiles[b, side][:, first - side * ROW : last - side * ROW],
+                    scalar=1.0 - ALPHA,
+                    in1=part,
+                    op0=ALU.mult,
+                    op1=ALU.add,
+                )
+                if last == ROW:
                     store(b, 0, last)
-                if side > 0 and last % WIDE == 0 and done < HALVES - PIECES:
+                if side > 0 and last % WIDE == 0:
                     store(b, last - WIDE, last)

from contextlib import ExitStack

import concourse.mybir as mybir
from concourse.masks import make_identity

F32 = mybir.dt.float32
BF16 = mybir.dt.bfloat16
I32 = mybir.dt.int32
U32 = mybir.dt.uint32
U8 = mybir.dt.uint8
FP8X4 = mybir.dt.float8_e4m3fn_x4
ALU = mybir.AluOpType
ACT = mybir.ActivationFunctionType

P = 128
PACK = 4
K_PASS = P * PACK
BANK = 512

BATCH = 256
B_TILES = BATCH // P
D = 8192
HIDDEN = 512
ALPHA = 1.0 / 10.0

WIDE = 2048
STEPS = D // WIDE
GROUPS = WIDE // K_PASS
ROW = 2 * WIDE
HALF = 2 * BANK
HALVES = B_TILES * D // HALF
HALVES_PER_SLAB = B_TILES * WIDE // HALF
PIECES = WIDE // HALF
RING = 12
LAG = 2
VECTOR_HALVES = 8
QUADS = 4
ROWS = 4

FLOPS = 2 * BATCH * D * HIDDEN * 3


def quantise_pair(nc, flip_pool, stage, ident_f32, pair, codes, plane):
    flipped = flip_pool.tile([P, 2, 2, P], F32, name="flipped", tag="flip")
    for i, rows in enumerate(pair):
        words = rows.bitcast(F32)
        for u in range(2):
            nc.tensor.transpose(flipped[:, i, u, :], words[:, u : K_PASS // 2 : 2], ident_f32)
    grouped = stage.tile([P, 2, P, PACK], BF16, name="grouped", align_bytes=64)
    nc.scalar.copy(
        out=grouped[:].rearrange("p i r t -> p (i r t)").bitcast(F32).rearrange("p (i r u) -> p i r u", i=2, u=2),
        in_=flipped[:].rearrange("p i u r -> p i r u"),
    )
    nc.vector.quantize_mx(
        out=codes.bitcast(FP8X4), scales=plane, in_=grouped[:].rearrange("p i r t -> p (i r t)")
    )


def tile_pecircuits_pb_k_kernel(
    tc,
    x_batch,
    predicted,
    r_som,
    r_neg_batch,
    W_pv1_ff_words,
    W_pv1_ff_scales,
    W_inh_pe_neg_words,
    W_inh_pe_neg_scales,
    W_som_dend_words,
    W_som_dend_scales,
    out,
):
    nc = tc.nc
    inh_view = W_inh_pe_neg_words[0].rearrange("p n t -> p (n t)")
    som_view = W_som_dend_words[0].rearrange("p n t -> p (n t)")

    with ExitStack() as ctx:
        ctx.enter_context(tc.manual_schedule())
        keep = ctx.enter_context(tc.tile_pool(name="keep", bufs=1))
        ring = ctx.enter_context(tc.tile_pool(name="ring", bufs=RING))
        stage = ctx.enter_context(tc.tile_pool(name="stage", bufs=3))
        sum1_pool = ctx.enter_context(tc.psum_pool(name="sum1_pool", bufs=1))
        flip_pool = ctx.enter_context(tc.psum_pool(name="flip_pool", bufs=3))
        sum2_pool = ctx.enter_context(tc.psum_pool(name="sum2_pool", bufs=3))

        ff_planes = keep.tile([P, STEPS, HIDDEN], U8, name="ff_planes", align_bytes=64)
        inh_planes = keep.tile([P, WIDE], U8, name="inh_planes", align_bytes=64)
        som_planes = keep.tile([P, WIDE], U8, name="som_planes", align_bytes=64)
        nc.vector.memset(ff_planes[:].bitcast(I32), 0)
        nc.vector.memset(inh_planes[:].bitcast(I32), 0)
        nc.vector.memset(som_planes[:].bitcast(I32), 0)

        ident_f32 = keep.tile([P, P], F32, name="ident_f32")
        ident_bf16 = keep.tile([P, P], BF16, name="ident_bf16")
        make_identity(nc, ident_f32[:])
        make_identity(nc, ident_bf16[:])
        minus_ident = keep.tile([P, P], BF16, name="minus_ident")
        nc.vector.tensor_scalar_mul(out=minus_ident[:], in0=ident_bf16[:], scalar1=-1.0)

        x_tiles = {}
        pred_tiles = {}
        rneg_tiles = {}
        ff_tiles = {}
        weight_tiles = {}

        def load_x(b):
            x_tiles[b] = keep.tile([P, D], BF16, name="x_rows%d" % b)
            nc.sync.dma_start(out=x_tiles[b][:], in_=x_batch[b * P : (b + 1) * P, :])

        def load_rows(tiles, b, side, dram):
            nc.sync.dma_start(
                out=tiles[b, side][:], in_=dram[b * P : (b + 1) * P, side * ROW : (side + 1) * ROW]
            )

        def ring_rows(tiles, b, side):
            tiles[b, side] = ring.tile([P, ROW], BF16, name="rows", tag="ring", align_bytes=64)

        def ring_ff(s):
            ff_tiles[s] = ring.tile([P, GROUPS, HIDDEN], U32, name="ff_words", tag="ring", align_bytes=64)

        def ring_weights(j):
            som_words = ring.tile([P, WIDE], U32, name="som_words", tag="ring", align_bytes=64)
            inh_words = ring.tile([P, WIDE], U32, name="inh_words", tag="ring", align_bytes=64)
            weight_tiles[j] = (som_words, inh_words)

        def load_ff(s):
            nc.sync.dma_start(
                out=ff_tiles[s][:].bitcast(I32),
                in_=W_pv1_ff_words[s * GROUPS : (s + 1) * GROUPS].rearrange("g p n t -> p g (n t)").bitcast(I32),
            )

        def load_ff_scales(s):
            for quad in range(QUADS):
                nc.sync.dma_start(
                    out=ff_planes[32 * quad : 32 * quad + GROUPS * ROWS, s, :].bitcast(I32),
                    in_=W_pv1_ff_scales[
                        s * GROUPS : (s + 1) * GROUPS, quad * ROWS : (quad + 1) * ROWS, :
                    ].bitcast(I32),
                )

        def load_out_scales(quad):
            for planes, scales in ((som_planes, W_som_dend_scales), (inh_planes, W_inh_pe_neg_scales)):
                nc.sync.dma_start(
                    out=planes[32 * quad : 32 * quad + STEPS * ROWS, :].bitcast(I32),
                    in_=scales[0, quad * ROWS : (quad + 1) * ROWS, :]
                    .rearrange("r (h n) -> h r n", h=STEPS)
                    .bitcast(I32),
                )

        def load_weights(j):
            byte_cols = slice(j * WIDE * PACK, (j + 1) * WIDE * PACK)
            for words, view in zip(weight_tiles[j], (som_view, inh_view)):
                nc.sync.dma_start(out=words[:].bitcast(I32), in_=view[:, byte_cols].bitcast(I32))

        work = [keep.tile([P, D], F32, name="work%d" % b) for b in range(B_TILES)]

        def difference(b, first, last):
            nc.vector.tensor_tensor(
                out=work[b][:, first:last],
                in0=pred_tiles[b, 0][:, first:last],
                in1=x_tiles[b][:, first:last],
                op=ALU.subtract,
            )

        ring_ff(0)
        ring_rows(pred_tiles, 0, 0)
        for s in range(1, STEPS):
            ring_ff(s)
        ring_rows(pred_tiles, 1, 0)
        ring_weights(0)
        for b in range(B_TILES):
            ring_rows(rneg_tiles, b, 0)
        ring_weights(1)

        load_x(0)
        load_ff_scales(0)
        load_x(1)
        load_ff(0)
        som_rows = keep.tile([P, B_TILES, HIDDEN], BF16, name="som_rows")
        nc.sync.dma_start(out=som_rows[:], in_=r_som.rearrange("(b p) k -> p b k", p=P))
        load_ff_scales(1)
        load_rows(pred_tiles, 0, 0, predicted)
        load_ff_scales(2)
        load_ff(1)
        load_ff_scales(3)
        load_rows(pred_tiles, 1, 0, predicted)
        load_out_scales(0)
        load_out_scales(1)
        load_ff(2)
        load_out_scales(2)
        load_out_scales(3)
        load_ff(3)
        load_weights(0)
        load_rows(rneg_tiles, 0, 0, r_neg_batch)
        load_rows(rneg_tiles, 1, 0, r_neg_batch)
        load_weights(1)

        hidden_sum = [sum1_pool.tile([P, HIDDEN], F32, name="hidden_sum%d" % b) for b in range(B_TILES)]
        som_codes = keep.tile([P, BATCH], U32, name="som_codes", align_bytes=64)
        som_plane = keep.tile([P, BATCH], U8, name="som_plane", align_bytes=64)
        pv_codes = keep.tile([P, BATCH], U32, name="pv_codes", align_bytes=64)
        pv_plane = keep.tile([P, BATCH], U8, name="pv_plane", align_bytes=64)

        x_quantised = {}

        def quantise_x(b):
            for pair in range(0, D // K_PASS, 2):
                codes = stage.tile([P, 2 * P], U32, name="x_codes", bufs=D // K_PASS, align_bytes=64)
                plane = stage.tile([P, 2 * P], U8, name="x_plane", bufs=D // K_PASS, align_bytes=64)
                sets = [x_tiles[b][:, g * K_PASS : (g + 1) * K_PASS] for g in (pair, pair + 1)]
                quantise_pair(nc, flip_pool, stage, ident_f32[:], sets, codes[:], plane[:])
                x_quantised[b, pair // 2] = (codes, plane)

        def multiply_slab(s):
            for i in range(GROUPS):
                g = s * GROUPS + i
                code_cols = slice(g % 2 * P, (g % 2 + 1) * P)
                for b in range(B_TILES):
                    codes, plane = x_quantised[b, g // 2]
                    nc.tensor.matmul_mx(
                        out=hidden_sum[b][:],
                        lhsT=codes[:, code_cols].bitcast(FP8X4),
                        lhsT_scale=plane[:, code_cols],
                        rhs=ff_tiles[s][:, i, :].bitcast(FP8X4),
                        rhs_scale=ff_planes[ROWS * i : P, s, :],
                        start=(g == 0),
                        stop=(g == D // K_PASS - 1),
                    )

        for b in range(B_TILES):
            quantise_x(b)
        som_sets = [som_rows[:, b, :] for b in range(B_TILES)]
        quantise_pair(nc, flip_pool, stage, ident_f32[:], som_sets, som_codes[:], som_plane[:])
        difference(0, 0, WIDE)
        difference(0, WIDE, ROW)
        difference(1, 0, WIDE)
        difference(1, WIDE, ROW)
        for s in range(STEPS):
            multiply_slab(s)

        rates = [keep.tile([P, PACK, P], BF16, name="rates%d" % b) for b in range(B_TILES)]
        by_word = [hidden_sum[b][:].rearrange("r (p t) -> r t p", t=PACK) for b in range(B_TILES)]
        nc.scalar.activation(out=rates[0][:], in_=by_word[0], func=ACT.Relu)
        nc.vector.tensor_scalar_max(out=rates[1][:], in0=by_word[1], scalar1=0.0)
        turned = []
        for b in range(B_TILES):
            turned.append(flip_pool.tile([P, PACK, P], BF16, name="turned", tag="flip"))
            for t in range(PACK):
                nc.tensor.transpose(turned[b][:, t, :], rates[b][:, t, :], ident_bf16[:])
        pv_grouped = [keep.tile([P, P, PACK], BF16, name="pv_grouped%d" % b, align_bytes=64) for b in range(B_TILES)]
        nc.scalar.copy(out=pv_grouped[0][:], in_=turned[0][:].rearrange("p t r -> p r t"))
        for b in range(B_TILES):
            if b == 1:
                nc.vector.tensor_copy(out=pv_grouped[1][:], in_=turned[1][:].rearrange("p t r -> p r t"))
            batch_cols = slice(b * P, (b + 1) * P)
            nc.vector.quantize_mx(
                out=pv_codes[:, batch_cols].bitcast(FP8X4),
                scales=pv_plane[:, batch_cols],
                in_=pv_grouped[b][:].rearrange("p r t -> p (r t)"),
            )

        for b in range(B_TILES):
            ring_rows(pred_tiles, b, 1)
            load_rows(pred_tiles, b, 1, predicted)
        ring_weights(2)
        load_weights(2)
        ring_rows(rneg_tiles, 0, 1)
        load_rows(rneg_tiles, 0, 1, r_neg_batch)

        def place(k):
            j, rest = divmod(k, HALVES_PER_SLAB)
            b, h = divmod(rest, PIECES)
            return j, b, j * WIDE + h * HALF

        def store(b, first, last):
            nc.sync.dma_start(out=out[b * P : (b + 1) * P, first:last], in_=work[b][:, first:last])

        def difference_by_tensor(k):
            j, b, first = place(k)
            for start in range(first, first + HALF, BANK):
                side, row_first = divmod(start, ROW)
                gap = flip_pool.tile([P, BANK], F32, name="gap", tag="flip")
                nc.tensor.matmul(
                    out=gap[:],
                    lhsT=ident_bf16[:],
                    rhs=pred_tiles[b, side][:, row_first : row_first + BANK],
                    start=True,
                    stop=False,
                )
                nc.tensor.matmul(
                    out=gap[:], lhsT=minus_ident[:], rhs=x_tiles[b][:, start : start + BANK], start=False, stop=True
                )
                nc.scalar.copy(out=work[b][:, start : start + BANK], in_=gap[:])

        for k in range(HALVES + LAG):
            if k < HALVES:
                j, b, first = place(k)
                som_words, inh_words = weight_tiles[j]
                batch_cols = slice(b * P, (b + 1) * P)
                for start in range(first, first + HALF, BANK):
                    cols = slice(start - j * WIDE, start - j * WIDE + BANK)
                    inhibition = sum2_pool.tile([P, BANK], F32, name="inhibition")
                    nc.tensor.matmul_mx(
                        out=inhibition[:],
                        lhsT=som_codes[:, batch_cols].bitcast(FP8X4),
                        lhsT_scale=som_plane[:, batch_cols],
                        rhs=som_words[:, cols].bitcast(FP8X4),
                        rhs_scale=som_planes[ROWS * j : P, cols],
                        start=True,
                        stop=False,
                    )
                    nc.tensor.matmul_mx(
                        out=inhibition[:],
                        lhsT=pv_codes[:, batch_cols].bitcast(FP8X4),
                        lhsT_scale=pv_plane[:, batch_cols],
                        rhs=inh_words[:, cols].bitcast(FP8X4),
                        rhs_scale=inh_planes[ROWS * j : P, cols],
                        start=False,
                        stop=True,
                    )
                    part = work[b][:, start : start + BANK]
                    nc.vector.tensor_tensor(out=part, in0=part, in1=inhibition[:], op=ALU.subtract)
                if VECTOR_HALVES <= k + HALVES_PER_SLAB < HALVES:
                    difference_by_tensor(k + HALVES_PER_SLAB)
                if k == HALVES_PER_SLAB - 1:
                    ring_rows(rneg_tiles, 1, 1)
                    load_rows(rneg_tiles, 1, 1, r_neg_batch)
                    ring_weights(STEPS - 1)
                    load_weights(STEPS - 1)
                part = work[b][:, first : first + HALF]
                nc.scalar.activation(out=part, in_=part, func=ACT.Relu, scale=ALPHA)
            if k >= LAG:
                done = k - LAG
                j, b, first = place(done)
                side = first // ROW
                last = first + HALF
                part = work[b][:, first:last]
                nc.vector.scalar_tensor_tensor(
                    out=part,
                    in0=rneg_tiles[b, side][:, first - side * ROW : last - side * ROW],
                    scalar=1.0 - ALPHA,
                    in1=part,
                    op0=ALU.mult,
                    op1=ALU.add,
                )
                if last == ROW:
                    store(b, 0, last)
                if side > 0 and last % WIDE == 0:
                    store(b, last - WIDE, last)
